import numpy as np
import ml_dtypes

BF16 = ml_dtypes.bfloat16


def bf(x):
    return np.asarray(x, np.float32).astype(BF16)


def f32(x):
    return np.asarray(x, np.float32)


def f64(x):
    return np.asarray(x).astype(np.float64)


def striped(idx):
    return np.tile(idx.reshape(-1, 16).T, (8, 1))


E, K, C, U, S, N, Q = 4, 1024, 1024, 128, 2048, 1024, 16
H = N // E
R = K // U


def setup_inputs():
    return {
        "base": f32(np.random.standard_normal((C, S))),
        "state": bf(np.random.standard_normal((K, N))),
        "q": bf(np.random.choice(np.arange(Q), size=(E, K, C))),
        "scale": f32(np.random.uniform(0.001, 0.02, (E, U, C))),
        "zp": f32(np.random.choice(np.arange(Q), size=(E, U, C))),
        "offs": striped(np.random.permutation(S)[:N]),
    }


def reference(base, state, q, scale, zp, offs):
    idx = offs[:16].T.reshape(-1)
    x = f64(state)
    qq = f64(q)
    sc = f64(scale)
    zz = f64(zp)
    xs = x.reshape(R, U, N).sum(axis=0)
    out = f64(base).copy()
    for e in range(E):
        cols = slice(e * H, (e + 1) * H)
        w = qq[e] * np.tile(sc[e], (R, 1))
        nz = -(zz[e] * sc[e])
        main = w.T @ x[:, cols]
        corr = nz.T @ xs[:, cols]
        out[:, idx[cols]] = main + corr
    return out

@@ -1,0 +1,102 @@
+import concourse.masks as masks
+import concourse.mybir as mybir
+
+BF16, F32, U16 = mybir.dt.bfloat16, mybir.dt.float32, mybir.dt.uint16
+MULT, ADD = mybir.AluOpType.mult, mybir.AluOpType.add
+
+P = 128
+E, K, C, S, N = 4, 1024, 1024, 2048, 1024
+R = K // P
+H = N // E
+BLOCKS = C // P
+PAIR = 2 * P
+BANK = 2 * H
+
+FLOPS = 2 * C * N * (K + P)
+
+
+def tile_moewna16matmul_b_kernel(tc, base, state, q, scale, zp, offs, out):
+    nc = tc.nc
+    q_view = q.rearrange("e (r u) c -> e u r c", u=P)
+    state_view = state.rearrange("(r u) j -> u r j", u=P)
+    scale_view = scale.rearrange("e u c -> u e c")
+    zp_view = zp.rearrange("e u c -> u e c")
+
+    with (
+        tc.tile_pool(name="held", bufs=1) as held,
+        tc.tile_pool(name="work", bufs=2) as work,
+        tc.psum_pool(name="psum_xs", bufs=2) as psum_xs,
+        tc.psum_pool(name="psum_main", bufs=4) as psum_main,
+        tc.psum_pool(name="psum_corr", bufs=2) as psum_corr,
+    ):
+        offsets = held.tile([P, N // 16], U16, name="offsets")
+        nc.sync.dma_start(offsets[:], offs)
+
+        tokens = [held.tile([P, R, H], BF16, name=f"tokens{e}") for e in range(E)]
+        scales = [held.tile([P, E, PAIR], F32, name=f"scales{g}") for g in range(C // PAIR)]
+        zeros = [held.tile([P, E, PAIR], F32, name=f"zeros{g}") for g in range(C // PAIR)]
+        codes = [[held.tile([P, R, PAIR], BF16, name=f"codes{g}_{e}") for e in range(E)] for g in range(C // PAIR)]
+        windows = [held.tile([P, S], F32, name=f"window{b}") for b in range(BLOCKS)]
+
+        for g in range(C // PAIR):
+            columns = slice(g * PAIR, (g + 1) * PAIR)
+            nc.sync.dma_start(scales[g][:], scale_view[:, :, columns])
+            for e in range(E):
+                nc.sync.dma_start(codes[g][e][:], q_view[e, :, :, columns])
+                if g == 0:
+                    nc.sync.dma_start(tokens[e][:], state_view[:, :, e * H : (e + 1) * H])
+            nc.sync.dma_start(zeros[g][:], zp_view[:, :, columns])
+            for b in (2 * g, 2 * g + 1):
+                nc.sync.dma_start(windows[b][:], base[b * P : (b + 1) * P, :])
+
+        identity = held.tile([P, P], BF16, name="identity")
+        masks.make_identity(nc, identity[:])
+        xs = held.tile([P, N], BF16, name="xs")
+        for e in range(E):
+            xs_ps = psum_xs.tile([P, H], F32, name="xs_ps")
+            for r in range(R):
+                nc.tensor.matmul(xs_ps[:], identity[:], tokens[e][:, r, :], start=(r == 0), stop=(r == R - 1))
+            nc.scalar.copy(xs[:, e * H : (e + 1) * H], xs_ps[:])
+
+        def dequantize(b):
+            g = b // 2
+            columns = slice((b % 2) * P, (b % 2 + 1) * P)
+            w = work.tile([P, E, R, P], BF16, name="w")
+            for e in range(E):
+                nc.vector.tensor_tensor(
+                    w[:, e, :, :],
+                    codes[g][e][:, :, columns],
+                    scales[g][:, e : e + 1, columns].to_broadcast([P, R, P]),
+                    MULT,
+                )
+            nz = work.tile([P, E, P], BF16, name="nz")
+            nc.vector.scalar_tensor_tensor(nz[:], zeros[g][:, :, columns], -1.0, scales[g][:, :, columns], MULT, MULT)
+            return w, nz
+
+        def multiply(w, nz):
+            main = work.tile([P, N], F32, name="main")
+            corr = work.tile([P, N], F32, name="corr")
+            for bank in range(N // BANK):
+                main_ps = psum_main.tile([P, BANK], F32, name="main_ps")
+                corr_ps = psum_corr.tile([P, BANK], F32, name="corr_ps")
+                for e in (2 * bank, 2 * bank + 1):
+                    part = slice((e % 2) * H, (e % 2 + 1) * H)
+                    for r in range(R):
+                        nc.tensor.matmul(
+                            main_ps[:, part], w[:, e, r, :], tokens[e][:, r, :], start=(r == 0), stop=(r == R - 1)
+                        )
+                    nc.tensor.matmul(corr_ps[:, part], nz[:, e, :], xs[:, e * H : (e + 1) * H], start=True, stop=True)
+                nc.scalar.copy(main[:, bank * BANK : (bank + 1) * BANK], main_ps[:])
+                nc.scalar.copy(corr[:, bank * BANK : (bank + 1) * BANK], corr_ps[:])
+            return main, corr
+
+        def place(b, main, corr):
+            nc.vector.tensor_tensor(windows[b][:].indirect(offsets[:]), main[:], corr[:], ADD)
+            nc.sync.dma_start(out[b * P : (b + 1) * P, :], windows[b][:])
+
+        sums = multiply(*dequantize(0))
+        for b in range(1, BLOCKS):
+            weights = dequantize(b)
+            place(b - 1, *sums)
+            sums = multiply(*weights)
+        place(BLOCKS - 1, *sums)

@@ -11,6 +11,7 @@ H = N // E
 BLOCKS = C // P
 PAIR = 2 * P
 BANK = 2 * H
+GPSIMD_EXPERTS = 3
 
 FLOPS = 2 * C * N * (K + P)
 
@@ -25,6 +26,7 @@ def tile_moewna16matmul_b_kernel(tc, base, state, q, scale, zp, offs, out):
     with (
         tc.tile_pool(name="held", bufs=1) as held,
         tc.tile_pool(name="work", bufs=2) as work,
+        tc.tile_pool(name="weights", bufs=3) as weights_pool,
         tc.psum_pool(name="psum_xs", bufs=2) as psum_xs,
         tc.psum_pool(name="psum_main", bufs=4) as psum_main,
         tc.psum_pool(name="psum_corr", bufs=2) as psum_corr,
@@ -61,15 +63,16 @@ def tile_moewna16matmul_b_kernel(tc, base, state, q, scale, zp, offs, out):
         def dequantize(b):
             g = b // 2
             columns = slice((b % 2) * P, (b % 2 + 1) * P)
-            w = work.tile([P, E, R, P], BF16, name="w")
+            w = weights_pool.tile([P, E, R, P], BF16, name="w")
             for e in range(E):
-                nc.vector.tensor_tensor(
+                engine = nc.gpsimd if e < GPSIMD_EXPERTS else nc.vector
+                engine.tensor_tensor(
                     w[:, e, :, :],
                     codes[g][e][:, :, columns],
                     scales[g][:, e : e + 1, columns].to_broadcast([P, R, P]),
                     MULT,
                 )
-            nz = work.tile([P, E, P], BF16, name="nz")
+            nz = weights_pool.tile([P, E, P], BF16, name="nz")
             nc.vector.scalar_tensor_tensor(nz[:], zeros[g][:, :, columns], -1.0, scales[g][:, :, columns], MULT, MULT)
             return w, nz
 

@@ -11,7 +11,7 @@ H = N // E
 BLOCKS = C // P
 PAIR = 2 * P
 BANK = 2 * H
-GPSIMD_EXPERTS = 3
+GPSIMD_EXPERT = 0
 
 FLOPS = 2 * C * N * (K + P)
 
@@ -27,9 +27,7 @@ def tile_moewna16matmul_b_kernel(tc, base, state, q, scale, zp, offs, out):
         tc.tile_pool(name="held", bufs=1) as held,
         tc.tile_pool(name="work", bufs=2) as work,
         tc.tile_pool(name="weights", bufs=3) as weights_pool,
-        tc.psum_pool(name="psum_xs", bufs=2) as psum_xs,
-        tc.psum_pool(name="psum_main", bufs=4) as psum_main,
-        tc.psum_pool(name="psum_corr", bufs=2) as psum_corr,
+        tc.psum_pool(name="psum", bufs=2) as psum,
     ):
         offsets = held.tile([P, N // 16], U16, name="offsets")
         nc.sync.dma_start(offsets[:], offs)
@@ -53,43 +51,66 @@ def tile_moewna16matmul_b_kernel(tc, base, state, q, scale, zp, offs, out):
 
         identity = held.tile([P, P], BF16, name="identity")
         masks.make_identity(nc, identity[:])
-        xs = held.tile([P, N], BF16, name="xs")
-        for e in range(E):
-            xs_ps = psum_xs.tile([P, H], F32, name="xs_ps")
-            for r in range(R):
-                nc.tensor.matmul(xs_ps[:], identity[:], tokens[e][:, r, :], start=(r == 0), stop=(r == R - 1))
-            nc.scalar.copy(xs[:, e * H : (e + 1) * H], xs_ps[:])
+        identity32 = held.tile([P, P], F32, name="identity32")
+        masks.make_identity(nc, identity32[:])
 
-        def dequantize(b):
+        def scale_to_psum(b):
+            scale_ps = psum.tile([P, E, P], F32, name="scale_ps")
+            nc.tensor.matmul(
+                scale_ps[:], identity32[:], scales[b // 2][:, :, (b % 2) * P : (b % 2 + 1) * P], start=True, stop=True
+            )
+            return scale_ps
+
+        def dequantize(b, scale_ps):
             g = b // 2
             columns = slice((b % 2) * P, (b % 2 + 1) * P)
             w = weights_pool.tile([P, E, R, P], BF16, name="w")
-            for e in range(E):
-                engine = nc.gpsimd if e < GPSIMD_EXPERTS else nc.vector
-                engine.tensor_tensor(
-                    w[:, e, :, :],
-                    codes[g][e][:, :, columns],
-                    scales[g][:, e : e + 1, columns].to_broadcast([P, R, P]),
-                    MULT,
-                )
             nz = weights_pool.tile([P, E, P], BF16, name="nz")
-            nc.vector.scalar_tensor_tensor(nz[:], zeros[g][:, :, columns], -1.0, scales[g][:, :, columns], MULT, MULT)
+            for e in range(E):
+                if e == GPSIMD_EXPERT:
+                    nc.gpsimd.tensor_tensor(
+                        w[:, e, :, :],
+                        codes[g][e][:, :, columns],
+                        scales[g][:, e : e + 1, columns].to_broadcast([P, R, P]),
+                        MULT,
+                    )
+                else:
+                    nc.vector.tensor_tensor(
+                        w[:, e, :, :],
+                        codes[g][e][:, :, columns],
+                        scale_ps[:, e : e + 1, :].to_broadcast([P, R, P]),
+                        MULT,
+                    )
+            minus_zp = weights_pool.tile([P, E, P], F32, name="minus_zp")
+            nc.scalar.mul(minus_zp[:], zeros[g][:, :, columns], -1.0)
+            nc.gpsimd.tensor_tensor(nz[:], minus_zp[:], scales[g][:, :, columns], MULT)
             return w, nz
 
         def multiply(w, nz):
             main = work.tile([P, N], F32, name="main")
             corr = work.tile([P, N], F32, name="corr")
             for bank in range(N // BANK):
-                main_ps = psum_main.tile([P, BANK], F32, name="main_ps")
-                corr_ps = psum_corr.tile([P, BANK], F32, name="corr_ps")
+                main_ps = psum.tile([P, BANK], F32, name="main_ps")
                 for e in (2 * bank, 2 * bank + 1):
-                    part = slice((e % 2) * H, (e % 2 + 1) * H)
                     for r in range(R):
                         nc.tensor.matmul(
-                            main_ps[:, part], w[:, e, r, :], tokens[e][:, r, :], start=(r == 0), stop=(r == R - 1)
+                            main_ps[:, (e % 2) * H : (e % 2 + 1) * H],
+                            w[:, e, r, :],
+                            tokens[e][:, r, :],
+                            start=(r == 0),
+                            stop=(r == R - 1),
                         )
-                    nc.tensor.matmul(corr_ps[:, part], nz[:, e, :], xs[:, e * H : (e + 1) * H], start=True, stop=True)
                 nc.scalar.copy(main[:, bank * BANK : (bank + 1) * BANK], main_ps[:])
+            for bank in range(N // BANK):
+                corr_ps = psum.tile([P, BANK], F32, name="corr_ps")
+                for e in (2 * bank, 2 * bank + 1):
+                    nc.tensor.matmul(
+                        corr_ps[:, (e % 2) * H : (e % 2 + 1) * H],
+                        nz[:, e, :],
+                        xs[:, e * H : (e + 1) * H],
+                        start=True,
+                        stop=True,
+                    )
                 nc.scalar.copy(corr[:, bank * BANK : (bank + 1) * BANK], corr_ps[:])
             return main, corr
 
@@ -97,9 +118,27 @@ def tile_moewna16matmul_b_kernel(tc, base, state, q, scale, zp, offs, out):
             nc.vector.tensor_tensor(windows[b][:].indirect(offsets[:]), main[:], corr[:], ADD)
             nc.sync.dma_start(out[b * P : (b + 1) * P, :], windows[b][:])
 
-        sums = multiply(*dequantize(0))
+        scale_now, scale_next = scale_to_psum(0), scale_to_psum(1)
+
+        xs = held.tile([P, N], BF16, name="xs")
+        for bank in range(N // BANK):
+            xs_ps = psum.tile([P, BANK], F32, name="xs_ps")
+            for e in (2 * bank, 2 * bank + 1):
+                for r in range(R):
+                    nc.tensor.matmul(
+                        xs_ps[:, (e % 2) * H : (e % 2 + 1) * H],
+                        identity[:],
+                        tokens[e][:, r, :],
+                        start=(r == 0),
+                        stop=(r == R - 1),
+                    )
+            nc.scalar.copy(xs[:, bank * BANK : (bank + 1) * BANK], xs_ps[:])
+
+        sums = multiply(*dequantize(0, scale_now))
         for b in range(1, BLOCKS):
-            weights = dequantize(b)
+            weights = dequantize(b, scale_next)
             place(b - 1, *sums)
+            if b + 1 < BLOCKS:
+                scale_next = scale_to_psum(b + 1)
             sums = multiply(*weights)
         place(BLOCKS - 1, *sums)

@@ -41,11 +41,11 @@ def tile_moewna16matmul_b_kernel(tc, base, state, q, scale, zp, offs, out):
         for g in range(C // PAIR):
             columns = slice(g * PAIR, (g + 1) * PAIR)
             nc.sync.dma_start(scales[g][:], scale_view[:, :, columns])
+            nc.sync.dma_start(zeros[g][:], zp_view[:, :, columns])
             for e in range(E):
                 nc.sync.dma_start(codes[g][e][:], q_view[e, :, :, columns])
                 if g == 0:
                     nc.sync.dma_start(tokens[e][:], state_view[:, :, e * H : (e + 1) * H])
-            nc.sync.dma_start(zeros[g][:], zp_view[:, :, columns])
             for b in (2 * g, 2 * g + 1):
                 nc.sync.dma_start(windows[b][:], base[b * P : (b + 1) * P, :])
 

@@ -41,11 +41,11 @@ def tile_moewna16matmul_b_kernel(tc, base, state, q, scale, zp, offs, out):
         for g in range(C // PAIR):
             columns = slice(g * PAIR, (g + 1) * PAIR)
             nc.sync.dma_start(scales[g][:], scale_view[:, :, columns])
-            nc.sync.dma_start(zeros[g][:], zp_view[:, :, columns])
             for e in range(E):
                 nc.sync.dma_start(codes[g][e][:], q_view[e, :, :, columns])
                 if g == 0:
                     nc.sync.dma_start(tokens[e][:], state_view[:, :, e * H : (e + 1) * H])
+            nc.sync.dma_start(zeros[g][:], zp_view[:, :, columns])
             for b in (2 * g, 2 * g + 1):
                 nc.sync.dma_start(windows[b][:], base[b * P : (b + 1) * P, :])
 
@@ -86,12 +86,22 @@ def tile_moewna16matmul_b_kernel(tc, base, state, q, scale, zp, offs, out):
             nc.gpsimd.tensor_tensor(nz[:], minus_zp[:], scales[g][:, :, columns], MULT)
             return w, nz
 
-        def multiply(w, nz):
+        xs = held.tile([P, N], BF16, name="xs")
+
+        def add_up_tokens(e):
+            xs_ps = psum.tile([P, H], F32, name="xs_ps")
+            for r in range(R):
+                nc.tensor.matmul(xs_ps[:], identity[:], tokens[e][:, r, :], start=(r == 0), stop=(r == R - 1))
+            nc.scalar.copy(xs[:, e * H : (e + 1) * H], xs_ps[:])
+
+        def multiply(b, w, nz):
             main = work.tile([P, N], F32, name="main")
             corr = work.tile([P, N], F32, name="corr")
             for bank in range(N // BANK):
                 main_ps = psum.tile([P, BANK], F32, name="main_ps")
                 for e in (2 * bank, 2 * bank + 1):
+                    if b == 0:
+                        add_up_tokens(e)
                     for r in range(R):
                         nc.tensor.matmul(
                             main_ps[:, (e % 2) * H : (e % 2 + 1) * H],
@@ -120,25 +130,11 @@ def tile_moewna16matmul_b_kernel(tc, base, state, q, scale, zp, offs, out):
 
         scale_now, scale_next = scale_to_psum(0), scale_to_psum(1)
 
-        xs = held.tile([P, N], BF16, name="xs")
-        for bank in range(N // BANK):
-            xs_ps = psum.tile([P, BANK], F32, name="xs_ps")
-            for e in (2 * bank, 2 * bank + 1):
-                for r in range(R):
-                    nc.tensor.matmul(
-                        xs_ps[:, (e % 2) * H : (e % 2 + 1) * H],
-                        identity[:],
-                        tokens[e][:, r, :],
-                        start=(r == 0),
-                        stop=(r == R - 1),
-                    )
-            nc.scalar.copy(xs[:, bank * BANK : (bank + 1) * BANK], xs_ps[:])
-
-        sums = multiply(*dequantize(0, scale_now))
+        sums = multiply(0, *dequantize(0, scale_now))
         for b in range(1, BLOCKS):
             weights = dequantize(b, scale_next)
             place(b - 1, *sums)
             if b + 1 < BLOCKS:
                 scale_next = scale_to_psum(b + 1)
-            sums = multiply(*weights)
+            sums = multiply(b, *weights)
         place(BLOCKS - 1, *sums)

@@ -38,13 +38,13 @@ def tile_moewna16matmul_b_kernel(tc, base, state, q, scale, zp, offs, out):
         codes = [[held.tile([P, R, PAIR], BF16, name=f"codes{g}_{e}") for e in range(E)] for g in range(C // PAIR)]
         windows = [held.tile([P, S], F32, name=f"window{b}") for b in range(BLOCKS)]
 
+        for e in range(E):
+            nc.sync.dma_start(tokens[e][:], state_view[:, :, e * H : (e + 1) * H])
         for g in range(C // PAIR):
             columns = slice(g * PAIR, (g + 1) * PAIR)
             nc.sync.dma_start(scales[g][:], scale_view[:, :, columns])
             for e in range(E):
                 nc.sync.dma_start(codes[g][e][:], q_view[e, :, :, columns])
-                if g == 0:
-                    nc.sync.dma_start(tokens[e][:], state_view[:, :, e * H : (e + 1) * H])
             nc.sync.dma_start(zeros[g][:], zp_view[:, :, columns])
             for b in (2 * g, 2 * g + 1):
                 nc.sync.dma_start(windows[b][:], base[b * P : (b + 1) * P, :])
@@ -86,22 +86,12 @@ def tile_moewna16matmul_b_kernel(tc, base, state, q, scale, zp, offs, out):
             nc.gpsimd.tensor_tensor(nz[:], minus_zp[:], scales[g][:, :, columns], MULT)
             return w, nz
 
-        xs = held.tile([P, N], BF16, name="xs")
-
-        def add_up_tokens(e):
-            xs_ps = psum.tile([P, H], F32, name="xs_ps")
-            for r in range(R):
-                nc.tensor.matmul(xs_ps[:], identity[:], tokens[e][:, r, :], start=(r == 0), stop=(r == R - 1))
-            nc.scalar.copy(xs[:, e * H : (e + 1) * H], xs_ps[:])
-
-        def multiply(b, w, nz):
+        def multiply(w, nz):
             main = work.tile([P, N], F32, name="main")
             corr = work.tile([P, N], F32, name="corr")
             for bank in range(N // BANK):
                 main_ps = psum.tile([P, BANK], F32, name="main_ps")
                 for e in (2 * bank, 2 * bank + 1):
-                    if b == 0:
-                        add_up_tokens(e)
                     for r in range(R):
                         nc.tensor.matmul(
                             main_ps[:, (e % 2) * H : (e % 2 + 1) * H],
@@ -128,13 +118,27 @@ def tile_moewna16matmul_b_kernel(tc, base, state, q, scale, zp, offs, out):
             nc.vector.tensor_tensor(windows[b][:].indirect(offsets[:]), main[:], corr[:], ADD)
             nc.sync.dma_start(out[b * P : (b + 1) * P, :], windows[b][:])
 
+        xs = held.tile([P, N], BF16, name="xs")
+        for bank in range(N // BANK):
+            xs_ps = psum.tile([P, BANK], F32, name="xs_ps")
+            for e in (2 * bank, 2 * bank + 1):
+                for r in range(R):
+                    nc.tensor.matmul(
+                        xs_ps[:, (e % 2) * H : (e % 2 + 1) * H],
+                        identity[:],
+                        tokens[e][:, r, :],
+                        start=(r == 0),
+                        stop=(r == R - 1),
+                    )
+            nc.scalar.copy(xs[:, bank * BANK : (bank + 1) * BANK], xs_ps[:])
+
         scale_now, scale_next = scale_to_psum(0), scale_to_psum(1)
 
-        sums = multiply(0, *dequantize(0, scale_now))
+        sums = multiply(*dequantize(0, scale_now))
         for b in range(1, BLOCKS):
             weights = dequantize(b, scale_next)
             place(b - 1, *sums)
             if b + 1 < BLOCKS:
                 scale_next = scale_to_psum(b + 1)
-            sums = multiply(b, *weights)
+            sums = multiply(*weights)
         place(BLOCKS - 1, *sums)

@@ -10,8 +10,12 @@ R = K // P
 H = N // E
 BLOCKS = C // P
 PAIR = 2 * P
+PAIRS = C // PAIR
 BANK = 2 * H
 GPSIMD_EXPERT = 0
+PAIRS_AHEAD = 2
+SCALES_AHEAD = 4
+WINDOWS_AHEAD = 3
 
 FLOPS = 2 * C * N * (K + P)
 
@@ -25,77 +29,78 @@ def tile_moewna16matmul_b_kernel(tc, base, state, q, scale, zp, offs, out):
 
     with (
         tc.tile_pool(name="held", bufs=1) as held,
-        tc.tile_pool(name="work", bufs=2) as work,
+        tc.tile_pool(name="codes", bufs=PAIRS_AHEAD * E) as codes_pool,
         tc.tile_pool(name="weights", bufs=3) as weights_pool,
+        tc.tile_pool(name="negated", bufs=2) as negated_pool,
+        tc.tile_pool(name="sums", bufs=BLOCKS) as sums_pool,
+        tc.tile_pool(name="windows", bufs=WINDOWS_AHEAD) as windows_pool,
+        tc.psum_pool(name="scale_psum", bufs=SCALES_AHEAD) as scale_psum,
         tc.psum_pool(name="psum", bufs=2) as psum,
     ):
         offsets = held.tile([P, N // 16], U16, name="offsets")
         nc.sync.dma_start(offsets[:], offs)
 
         tokens = [held.tile([P, R, H], BF16, name=f"tokens{e}") for e in range(E)]
-        scales = [held.tile([P, E, PAIR], F32, name=f"scales{g}") for g in range(C // PAIR)]
-        zeros = [held.tile([P, E, PAIR], F32, name=f"zeros{g}") for g in range(C // PAIR)]
-        codes = [[held.tile([P, R, PAIR], BF16, name=f"codes{g}_{e}") for e in range(E)] for g in range(C // PAIR)]
-        windows = [held.tile([P, S], F32, name=f"window{b}") for b in range(BLOCKS)]
+        scales = [held.tile([P, E, PAIR], F32, name=f"scales{g}") for g in range(PAIRS)]
+        zeros = [held.tile([P, E, PAIR], F32, name=f"zeros{g}") for g in range(PAIRS)]
 
-        for e in range(E):
-            nc.sync.dma_start(tokens[e][:], state_view[:, :, e * H : (e + 1) * H])
-        for g in range(C // PAIR):
+        def fetch_pair(g):
             columns = slice(g * PAIR, (g + 1) * PAIR)
             nc.sync.dma_start(scales[g][:], scale_view[:, :, columns])
+            codes = []
             for e in range(E):
-                nc.sync.dma_start(codes[g][e][:], q_view[e, :, :, columns])
+                codes.append(codes_pool.tile([P, R, PAIR], BF16, name="codes"))
+                nc.sync.dma_start(codes[e][:], q_view[e, :, :, columns])
             nc.sync.dma_start(zeros[g][:], zp_view[:, :, columns])
-            for b in (2 * g, 2 * g + 1):
-                nc.sync.dma_start(windows[b][:], base[b * P : (b + 1) * P, :])
+            return codes
 
-        identity = held.tile([P, P], BF16, name="identity")
-        masks.make_identity(nc, identity[:])
-        identity32 = held.tile([P, P], F32, name="identity32")
-        masks.make_identity(nc, identity32[:])
+        def fetch_window(b):
+            window = windows_pool.tile([P, S], F32, name="window")
+            nc.sync.dma_start(window[:], base[b * P : (b + 1) * P, :])
+            return window
 
         def scale_to_psum(b):
-            scale_ps = psum.tile([P, E, P], F32, name="scale_ps")
+            scale_ps = scale_psum.tile([P, E, P], F32, name="scale_ps")
             nc.tensor.matmul(
                 scale_ps[:], identity32[:], scales[b // 2][:, :, (b % 2) * P : (b % 2 + 1) * P], start=True, stop=True
             )
             return scale_ps
 
-        def dequantize(b, scale_ps):
-            g = b // 2
-            columns = slice((b % 2) * P, (b % 2 + 1) * P)
-            w = weights_pool.tile([P, E, R, P], BF16, name="w")
-            nz = weights_pool.tile([P, E, P], BF16, name="nz")
-            for e in range(E):
-                if e == GPSIMD_EXPERT:
-                    nc.gpsimd.tensor_tensor(
-                        w[:, e, :, :],
-                        codes[g][e][:, :, columns],
-                        scales[g][:, e : e + 1, columns].to_broadcast([P, R, P]),
-                        MULT,
-                    )
-                else:
-                    nc.vector.tensor_tensor(
-                        w[:, e, :, :],
-                        codes[g][e][:, :, columns],
-                        scale_ps[:, e : e + 1, :].to_broadcast([P, R, P]),
-                        MULT,
-                    )
-            minus_zp = weights_pool.tile([P, E, P], F32, name="minus_zp")
-            nc.scalar.mul(minus_zp[:], zeros[g][:, :, columns], -1.0)
-            nc.gpsimd.tensor_tensor(nz[:], minus_zp[:], scales[g][:, :, columns], MULT)
+        def dequantize(g, codes, scale_ps_of_half):
+            w = weights_pool.tile([P, E, R, PAIR], BF16, name="w")
+            nz = weights_pool.tile([P, E, PAIR], BF16, name="nz")
+            nc.gpsimd.tensor_tensor(
+                w[:, GPSIMD_EXPERT, :, :],
+                codes[GPSIMD_EXPERT][:],
+                scales[g][:, GPSIMD_EXPERT : GPSIMD_EXPERT + 1, :].to_broadcast([P, R, PAIR]),
+                MULT,
+            )
+            minus_zp = negated_pool.tile([P, E, PAIR], F32, name="minus_zp")
+            nc.scalar.mul(minus_zp[:], zeros[g][:], -1.0)
+            nc.gpsimd.tensor_tensor(nz[:], minus_zp[:], scales[g][:], MULT)
+            for half in range(2):
+                columns = slice(half * P, (half + 1) * P)
+                for e in range(E):
+                    if e != GPSIMD_EXPERT:
+                        nc.vector.tensor_tensor(
+                            w[:, e, :, columns],
+                            codes[e][:, :, columns],
+                            scale_ps_of_half[half][:, e : e + 1, :].to_broadcast([P, R, P]),
+                            MULT,
+                        )
             return w, nz
 
-        def multiply(w, nz):
-            main = work.tile([P, N], F32, name="main")
-            corr = work.tile([P, N], F32, name="corr")
+        def multiply(b, w, nz):
+            columns = slice((b % 2) * P, (b % 2 + 1) * P)
+            main = sums_pool.tile([P, N], F32, name="main")
+            corr = sums_pool.tile([P, N], F32, name="corr")
             for bank in range(N // BANK):
                 main_ps = psum.tile([P, BANK], F32, name="main_ps")
                 for e in (2 * bank, 2 * bank + 1):
                     for r in range(R):
                         nc.tensor.matmul(
                             main_ps[:, (e % 2) * H : (e % 2 + 1) * H],
-                            w[:, e, r, :],
+                            w[:, e, r, columns],
                             tokens[e][:, r, :],
                             start=(r == 0),
                             stop=(r == R - 1),
@@ -106,7 +111,7 @@ def tile_moewna16matmul_b_kernel(tc, base, state, q, scale, zp, offs, out):
                 for e in (2 * bank, 2 * bank + 1):
                     nc.tensor.matmul(
                         corr_ps[:, (e % 2) * H : (e % 2 + 1) * H],
-                        nz[:, e, :],
+                        nz[:, e, columns],
                         xs[:, e * H : (e + 1) * H],
                         start=True,
                         stop=True,
@@ -114,13 +119,21 @@ def tile_moewna16matmul_b_kernel(tc, base, state, q, scale, zp, offs, out):
                 nc.scalar.copy(corr[:, bank * BANK : (bank + 1) * BANK], corr_ps[:])
             return main, corr
 
-        def place(b, main, corr):
-            nc.vector.tensor_tensor(windows[b][:].indirect(offsets[:]), main[:], corr[:], ADD)
-            nc.sync.dma_start(out[b * P : (b + 1) * P, :], windows[b][:])
+        codes_of_pair = {0: fetch_pair(0)}
+        for e in range(E):
+            nc.sync.dma_start(tokens[e][:], state_view[:, :, e * H : (e + 1) * H])
+        codes_of_pair[1] = fetch_pair(1)
+
+        identity = held.tile([P, P], BF16, name="identity")
+        masks.make_identity(nc, identity[:])
+        identity32 = held.tile([P, P], F32, name="identity32")
+        masks.make_identity(nc, identity32[:])
+
+        scale_ps_of_block = {b: scale_to_psum(b) for b in range(SCALES_AHEAD)}
 
         xs = held.tile([P, N], BF16, name="xs")
         for bank in range(N // BANK):
-            xs_ps = psum.tile([P, BANK], F32, name="xs_ps")
+            xs_ps = psum.tile([P, BANK], F32, name="xs_ps", tag="corr_ps")
             for e in (2 * bank, 2 * bank + 1):
                 for r in range(R):
                     nc.tensor.matmul(
@@ -132,13 +145,21 @@ def tile_moewna16matmul_b_kernel(tc, base, state, q, scale, zp, offs, out):
                     )
             nc.scalar.copy(xs[:, bank * BANK : (bank + 1) * BANK], xs_ps[:])
 
-        scale_now, scale_next = scale_to_psum(0), scale_to_psum(1)
+        sums = []
+        for g in range(PAIRS):
+            w, nz = dequantize(g, codes_of_pair[g], (scale_ps_of_block[2 * g], scale_ps_of_block[2 * g + 1]))
+            if g + PAIRS_AHEAD < PAIRS:
+                codes_of_pair[g + PAIRS_AHEAD] = fetch_pair(g + PAIRS_AHEAD)
+            for b in (2 * g, 2 * g + 1):
+                if b + SCALES_AHEAD < BLOCKS:
+                    scale_ps_of_block[b + SCALES_AHEAD] = scale_to_psum(b + SCALES_AHEAD)
+            for b in (2 * g, 2 * g + 1):
+                sums.append(multiply(b, w, nz))
 
-        sums = multiply(*dequantize(0, scale_now))
-        for b in range(1, BLOCKS):
-            weights = dequantize(b, scale_next)
-            place(b - 1, *sums)
-            if b + 1 < BLOCKS:
-                scale_next = scale_to_psum(b + 1)
-            sums = multiply(*weights)
-        place(BLOCKS - 1, *sums)
+        windows = {b: fetch_window(b) for b in range(WINDOWS_AHEAD)}
+        for b in range(BLOCKS):
+            main, corr = sums[b]
+            nc.vector.tensor_tensor(windows[b][:].indirect(offsets[:]), main[:], corr[:], ADD)
+            nc.sync.dma_start(out[b * P : (b + 1) * P, :], windows[b][:])
+            if b + WINDOWS_AHEAD < BLOCKS:
+                windows[b + WINDOWS_AHEAD] = fetch_window(b + WINDOWS_AHEAD)

@@ -9,13 +9,13 @@ E, K, C, S, N = 4, 1024, 1024, 2048, 1024
 R = K // P
 H = N // E
 BLOCKS = C // P
-PAIR = 2 * P
-PAIRS = C // PAIR
+HALF = C // 2
+HALVES = C // HALF
+RH = R // 2
 BANK = 2 * H
-GPSIMD_EXPERT = 0
-PAIRS_AHEAD = 2
-SCALES_AHEAD = 4
-WINDOWS_AHEAD = 3
+GPSIMD_EXPERT = 1
+VECTOR_EXPERTS = [e for e in range(E) if e != GPSIMD_EXPERT]
+SUMS_AHEAD = 4
 
 FLOPS = 2 * C * N * (K + P)
 
@@ -29,69 +29,63 @@ def tile_moewna16matmul_b_kernel(tc, base, state, q, scale, zp, offs, out):
 
     with (
         tc.tile_pool(name="held", bufs=1) as held,
-        tc.tile_pool(name="codes", bufs=PAIRS_AHEAD * E) as codes_pool,
-        tc.tile_pool(name="weights", bufs=3) as weights_pool,
-        tc.tile_pool(name="negated", bufs=2) as negated_pool,
-        tc.tile_pool(name="sums", bufs=BLOCKS) as sums_pool,
-        tc.tile_pool(name="windows", bufs=WINDOWS_AHEAD) as windows_pool,
-        tc.psum_pool(name="scale_psum", bufs=SCALES_AHEAD) as scale_psum,
+        tc.tile_pool(name="streamed", bufs=BLOCKS) as streamed,
+        tc.tile_pool(name="sums", bufs=SUMS_AHEAD) as sums_pool,
+        tc.psum_pool(name="scale_psum", bufs=4) as scale_psum,
         tc.psum_pool(name="psum", bufs=2) as psum,
     ):
         offsets = held.tile([P, N // 16], U16, name="offsets")
         nc.sync.dma_start(offsets[:], offs)
 
-        tokens = [held.tile([P, R, H], BF16, name=f"tokens{e}") for e in range(E)]
-        scales = [held.tile([P, E, PAIR], F32, name=f"scales{g}") for g in range(PAIRS)]
-        zeros = [held.tile([P, E, PAIR], F32, name=f"zeros{g}") for g in range(PAIRS)]
+        tokens = held.tile([P, R, N], BF16, name="tokens")
+        scales = [held.tile([P, E, HALF], F32, name=f"scales{h}") for h in range(HALVES)]
+        minus_zp = [held.tile([P, E, HALF], F32, name=f"minus_zp{h}") for h in range(HALVES)]
+        w = [held.tile([P, E, R, HALF], BF16, name=f"w{h}") for h in range(HALVES)]
+        nz = [held.tile([P, E, HALF], BF16, name=f"nz{h}") for h in range(HALVES)]
+        codes = [
+            [streamed.tile([P, R, HALF], BF16, name="codes", tag="streamed") for e in range(E)] for h in range(HALVES)
+        ]
 
-        def fetch_pair(g):
-            columns = slice(g * PAIR, (g + 1) * PAIR)
-            nc.sync.dma_start(scales[g][:], scale_view[:, :, columns])
-            codes = []
-            for e in range(E):
-                codes.append(codes_pool.tile([P, R, PAIR], BF16, name="codes"))
-                nc.sync.dma_start(codes[e][:], q_view[e, :, :, columns])
-            nc.sync.dma_start(zeros[g][:], zp_view[:, :, columns])
-            return codes
+        def fetch_half(h):
+            columns = slice(h * HALF, (h + 1) * HALF)
+            nc.sync.dma_start(scales[h][:], scale_view[:, :, columns])
+            for rows in (slice(0, RH), slice(RH, R)):
+                for e in range(E):
+                    nc.sync.dma_start(codes[h][e][:, rows, :], q_view[e, :, rows, columns])
+                    if e == GPSIMD_EXPERT and rows.stop == R:
+                        nc.sync.dma_start(minus_zp[h][:], zp_view[:, :, columns])
 
         def fetch_window(b):
-            window = windows_pool.tile([P, S], F32, name="window")
+            window = streamed.tile([P, S], F32, name="window", tag="streamed")
             nc.sync.dma_start(window[:], base[b * P : (b + 1) * P, :])
             return window
 
-        def scale_to_psum(b):
-            scale_ps = scale_psum.tile([P, E, P], F32, name="scale_ps")
-            nc.tensor.matmul(
-                scale_ps[:], identity32[:], scales[b // 2][:, :, (b % 2) * P : (b % 2 + 1) * P], start=True, stop=True
-            )
+        def scale_to_psum(h, e):
+            scale_ps = scale_psum.tile([P, 1, HALF], F32, name="scale_ps")
+            nc.tensor.matmul(scale_ps[:, 0, :], identity32[:], scales[h][:, e, :], start=True, stop=True)
             return scale_ps
 
-        def dequantize(g, codes, scale_ps_of_half):
-            w = weights_pool.tile([P, E, R, PAIR], BF16, name="w")
-            nz = weights_pool.tile([P, E, PAIR], BF16, name="nz")
-            nc.gpsimd.tensor_tensor(
-                w[:, GPSIMD_EXPERT, :, :],
-                codes[GPSIMD_EXPERT][:],
-                scales[g][:, GPSIMD_EXPERT : GPSIMD_EXPERT + 1, :].to_broadcast([P, R, PAIR]),
-                MULT,
-            )
-            minus_zp = negated_pool.tile([P, E, PAIR], F32, name="minus_zp")
-            nc.scalar.mul(minus_zp[:], zeros[g][:], -1.0)
-            nc.gpsimd.tensor_tensor(nz[:], minus_zp[:], scales[g][:], MULT)
-            for half in range(2):
-                columns = slice(half * P, (half + 1) * P)
-                for e in range(E):
-                    if e != GPSIMD_EXPERT:
-                        nc.vector.tensor_tensor(
-                            w[:, e, :, columns],
-                            codes[e][:, :, columns],
-                            scale_ps_of_half[half][:, e : e + 1, :].to_broadcast([P, R, P]),
-                            MULT,
-                        )
-            return w, nz
+        def dequantize(h, scale_ps_of_expert):
+            for rows in (slice(0, RH), slice(RH, R)):
+                nc.gpsimd.tensor_tensor(
+                    w[h][:, GPSIMD_EXPERT, rows, :],
+                    codes[h][GPSIMD_EXPERT][:, rows, :],
+                    scales[h][:, GPSIMD_EXPERT : GPSIMD_EXPERT + 1, :].to_broadcast([P, RH, HALF]),
+                    MULT,
+                )
+                for e in VECTOR_EXPERTS:
+                    nc.vector.tensor_tensor(
+                        w[h][:, e, rows, :],
+                        codes[h][e][:, rows, :],
+                        scale_ps_of_expert[e][:].to_broadcast([P, RH, HALF]),
+                        MULT,
+                    )
+            nc.scalar.mul(minus_zp[h][:], minus_zp[h][:], -1.0)
+            nc.gpsimd.tensor_tensor(nz[h][:], minus_zp[h][:], scales[h][:], MULT)
 
-        def multiply(b, w, nz):
-            columns = slice((b % 2) * P, (b % 2 + 1) * P)
+        def multiply(b):
+            h = b * P // HALF
+            columns = slice(b * P - h * HALF, (b + 1) * P - h * HALF)
             main = sums_pool.tile([P, N], F32, name="main")
             corr = sums_pool.tile([P, N], F32, name="corr")
             for bank in range(N // BANK):
@@ -100,8 +94,8 @@ def tile_moewna16matmul_b_kernel(tc, base, state, q, scale, zp, offs, out):
                     for r in range(R):
                         nc.tensor.matmul(
                             main_ps[:, (e % 2) * H : (e % 2 + 1) * H],
-                            w[:, e, r, columns],
-                            tokens[e][:, r, :],
+                            w[h][:, e, r, columns],
+                            tokens[:, r, e * H : (e + 1) * H],
                             start=(r == 0),
                             stop=(r == R - 1),
                         )
@@ -111,7 +105,7 @@ def tile_moewna16matmul_b_kernel(tc, base, state, q, scale, zp, offs, out):
                 for e in (2 * bank, 2 * bank + 1):
                     nc.tensor.matmul(
                         corr_ps[:, (e % 2) * H : (e % 2 + 1) * H],
-                        nz[:, e, columns],
+                        nz[h][:, e, columns],
                         xs[:, e * H : (e + 1) * H],
                         start=True,
                         stop=True,
@@ -119,47 +113,43 @@ def tile_moewna16matmul_b_kernel(tc, base, state, q, scale, zp, offs, out):
                 nc.scalar.copy(corr[:, bank * BANK : (bank + 1) * BANK], corr_ps[:])
             return main, corr
 
-        codes_of_pair = {0: fetch_pair(0)}
-        for e in range(E):
-            nc.sync.dma_start(tokens[e][:], state_view[:, :, e * H : (e + 1) * H])
-        codes_of_pair[1] = fetch_pair(1)
+        fetch_half(0)
+        nc.sync.dma_start(tokens[:], state_view)
+        fetch_half(1)
 
         identity = held.tile([P, P], BF16, name="identity")
         masks.make_identity(nc, identity[:])
         identity32 = held.tile([P, P], F32, name="identity32")
         masks.make_identity(nc, identity32[:])
 
-        scale_ps_of_block = {b: scale_to_psum(b) for b in range(SCALES_AHEAD)}
+        scale_ps = {h: {} for h in range(HALVES)}
+        for e in VECTOR_EXPERTS:
+            scale_ps[0][e] = scale_to_psum(0, e)
+        for h in range(HALVES):
+            dequantize(h, scale_ps[h])
+            if h + 1 < HALVES:
+                for e in VECTOR_EXPERTS:
+                    scale_ps[h + 1][e] = scale_to_psum(h + 1, e)
 
         xs = held.tile([P, N], BF16, name="xs")
         for bank in range(N // BANK):
             xs_ps = psum.tile([P, BANK], F32, name="xs_ps", tag="corr_ps")
-            for e in (2 * bank, 2 * bank + 1):
-                for r in range(R):
-                    nc.tensor.matmul(
-                        xs_ps[:, (e % 2) * H : (e % 2 + 1) * H],
-                        identity[:],
-                        tokens[e][:, r, :],
-                        start=(r == 0),
-                        stop=(r == R - 1),
-                    )
+            for r in range(R):
+                nc.tensor.matmul(
+                    xs_ps[:],
+                    identity[:],
+                    tokens[:, r, bank * BANK : (bank + 1) * BANK],
+                    start=(r == 0),
+                    stop=(r == R - 1),
+                )
             nc.scalar.copy(xs[:, bank * BANK : (bank + 1) * BANK], xs_ps[:])
 
-        sums = []
-        for g in range(PAIRS):
-            w, nz = dequantize(g, codes_of_pair[g], (scale_ps_of_block[2 * g], scale_ps_of_block[2 * g + 1]))
-            if g + PAIRS_AHEAD < PAIRS:
-                codes_of_pair[g + PAIRS_AHEAD] = fetch_pair(g + PAIRS_AHEAD)
-            for b in (2 * g, 2 * g + 1):
-                if b + SCALES_AHEAD < BLOCKS:
-                    scale_ps_of_block[b + SCALES_AHEAD] = scale_to_psum(b + SCALES_AHEAD)
-            for b in (2 * g, 2 * g + 1):
-                sums.append(multiply(b, w, nz))
+        sums = {b: multiply(b) for b in range(SUMS_AHEAD)}
 
-        windows = {b: fetch_window(b) for b in range(WINDOWS_AHEAD)}
+        windows = [fetch_window(b) for b in range(BLOCKS)]
         for b in range(BLOCKS):
             main, corr = sums[b]
             nc.vector.tensor_tensor(windows[b][:].indirect(offsets[:]), main[:], corr[:], ADD)
             nc.sync.dma_start(out[b * P : (b + 1) * P, :], windows[b][:])
-            if b + WINDOWS_AHEAD < BLOCKS:
-                windows[b + WINDOWS_AHEAD] = fetch_window(b + WINDOWS_AHEAD)
+            if b + SUMS_AHEAD < BLOCKS:
+                sums[b + SUMS_AHEAD] = multiply(b + SUMS_AHEAD)

@@ -12,8 +12,9 @@ BLOCKS = C // P
 HALF = C // 2
 HALVES = C // HALF
 RH = R // 2
+LOW, HIGH = slice(0, RH), slice(RH, R)
 BANK = 2 * H
-GPSIMD_EXPERT = 1
+GPSIMD_EXPERT = 0
 VECTOR_EXPERTS = [e for e in range(E) if e != GPSIMD_EXPERT]
 SUMS_AHEAD = 4
 
@@ -46,14 +47,8 @@ def tile_moewna16matmul_b_kernel(tc, base, state, q, scale, zp, offs, out):
             [streamed.tile([P, R, HALF], BF16, name="codes", tag="streamed") for e in range(E)] for h in range(HALVES)
         ]
 
-        def fetch_half(h):
-            columns = slice(h * HALF, (h + 1) * HALF)
-            nc.sync.dma_start(scales[h][:], scale_view[:, :, columns])
-            for rows in (slice(0, RH), slice(RH, R)):
-                for e in range(E):
-                    nc.sync.dma_start(codes[h][e][:, rows, :], q_view[e, :, rows, columns])
-                    if e == GPSIMD_EXPERT and rows.stop == R:
-                        nc.sync.dma_start(minus_zp[h][:], zp_view[:, :, columns])
+        def fetch_codes(h, e, rows):
+            nc.sync.dma_start(codes[h][e][:, rows, :], q_view[e, :, rows, h * HALF : (h + 1) * HALF])
 
         def fetch_window(b):
             window = streamed.tile([P, S], F32, name="window", tag="streamed")
@@ -66,7 +61,7 @@ def tile_moewna16matmul_b_kernel(tc, base, state, q, scale, zp, offs, out):
             return scale_ps
 
         def dequantize(h, scale_ps_of_expert):
-            for rows in (slice(0, RH), slice(RH, R)):
+            for rows in (LOW, HIGH):
                 nc.gpsimd.tensor_tensor(
                     w[h][:, GPSIMD_EXPERT, rows, :],
                     codes[h][GPSIMD_EXPERT][:, rows, :],
@@ -113,9 +108,17 @@ def tile_moewna16matmul_b_kernel(tc, base, state, q, scale, zp, offs, out):
                 nc.scalar.copy(corr[:, bank * BANK : (bank + 1) * BANK], corr_ps[:])
             return main, corr
 
-        fetch_half(0)
-        nc.sync.dma_start(tokens[:], state_view)
-        fetch_half(1)
+        for h in range(HALVES):
+            nc.sync.dma_start(scales[h][:], scale_view[:, :, h * HALF : (h + 1) * HALF])
+            fetch_codes(h, GPSIMD_EXPERT, LOW)
+            if h == 1:
+                nc.sync.dma_start(tokens[:], state_view)
+            for e in VECTOR_EXPERTS:
+                fetch_codes(h, e, LOW)
+            fetch_codes(h, GPSIMD_EXPERT, HIGH)
+            nc.sync.dma_start(minus_zp[h][:], zp_view[:, :, h * HALF : (h + 1) * HALF])
+            for e in VECTOR_EXPERTS:
+                fetch_codes(h, e, HIGH)
 
         identity = held.tile([P, P], BF16, name="identity")
         masks.make_identity(nc, identity[:])

@@ -16,6 +16,7 @@ LOW, HIGH = slice(0, RH), slice(RH, R)
 BANK = 2 * H
 GPSIMD_EXPERT = 0
 VECTOR_EXPERTS = [e for e in range(E) if e != GPSIMD_EXPERT]
+EXPERT_PAIRS = (slice(0, 2), slice(2, 4))
 SUMS_AHEAD = 4
 
 FLOPS = 2 * C * N * (K + P)
@@ -40,7 +41,8 @@ def tile_moewna16matmul_b_kernel(tc, base, state, q, scale, zp, offs, out):
 
         tokens = held.tile([P, R, N], BF16, name="tokens")
         scales = [held.tile([P, E, HALF], F32, name=f"scales{h}") for h in range(HALVES)]
-        minus_zp = [held.tile([P, E, HALF], F32, name=f"minus_zp{h}") for h in range(HALVES)]
+        minus_scales = [held.tile([P, E, HALF], F32, name=f"minus_scales{h}") for h in range(HALVES)]
+        zero_points = [held.tile([P, E, HALF], F32, name=f"zero_points{h}") for h in range(HALVES)]
         w = [held.tile([P, E, R, HALF], BF16, name=f"w{h}") for h in range(HALVES)]
         nz = [held.tile([P, E, HALF], BF16, name=f"nz{h}") for h in range(HALVES)]
         codes = [
@@ -49,6 +51,13 @@ def tile_moewna16matmul_b_kernel(tc, base, state, q, scale, zp, offs, out):
 
         def fetch_codes(h, e, rows):
             nc.sync.dma_start(codes[h][e][:, rows, :], q_view[e, :, rows, h * HALF : (h + 1) * HALF])
+
+        def fetch_zp(h, pair):
+            nc.sync.dma_start(zero_points[h][:, pair, :], zp_view[:, pair, h * HALF : (h + 1) * HALF])
+
+        def fetch_tokens(bank):
+            columns = slice(bank * BANK, (bank + 1) * BANK)
+            nc.sync.dma_start(tokens[:, :, columns], state_view[:, :, columns])
 
         def fetch_window(b):
             window = streamed.tile([P, S], F32, name="window", tag="streamed")
@@ -61,6 +70,7 @@ def tile_moewna16matmul_b_kernel(tc, base, state, q, scale, zp, offs, out):
             return scale_ps
 
         def dequantize(h, scale_ps_of_expert):
+            nc.scalar.mul(minus_scales[h][:], scales[h][:], -1.0)
             for rows in (LOW, HIGH):
                 nc.gpsimd.tensor_tensor(
                     w[h][:, GPSIMD_EXPERT, rows, :],
@@ -75,8 +85,8 @@ def tile_moewna16matmul_b_kernel(tc, base, state, q, scale, zp, offs, out):
                         scale_ps_of_expert[e][:].to_broadcast([P, RH, HALF]),
                         MULT,
                     )
-            nc.scalar.mul(minus_zp[h][:], minus_zp[h][:], -1.0)
-            nc.gpsimd.tensor_tensor(nz[h][:], minus_zp[h][:], scales[h][:], MULT)
+            for pair in EXPERT_PAIRS:
+                nc.gpsimd.tensor_tensor(nz[h][:, pair, :], zero_points[h][:, pair, :], minus_scales[h][:, pair, :], MULT)
 
         def multiply(b):
             h = b * P // HALF
@@ -109,16 +119,22 @@ def tile_moewna16matmul_b_kernel(tc, base, state, q, scale, zp, offs, out):
             return main, corr
 
         for h in range(HALVES):
+            first, second, third = VECTOR_EXPERTS
             nc.sync.dma_start(scales[h][:], scale_view[:, :, h * HALF : (h + 1) * HALF])
             fetch_codes(h, GPSIMD_EXPERT, LOW)
-            if h == 1:
-                nc.sync.dma_start(tokens[:], state_view)
-            for e in VECTOR_EXPERTS:
-                fetch_codes(h, e, LOW)
+            fetch_codes(h, first, LOW)
+            fetch_codes(h, second, LOW)
+            if h == HALVES - 1:
+                fetch_tokens(0)
             fetch_codes(h, GPSIMD_EXPERT, HIGH)
-            nc.sync.dma_start(minus_zp[h][:], zp_view[:, :, h * HALF : (h + 1) * HALF])
-            for e in VECTOR_EXPERTS:
-                fetch_codes(h, e, HIGH)
+            fetch_codes(h, third, LOW)
+            if h == HALVES - 1:
+                fetch_tokens(1)
+            fetch_codes(h, first, HIGH)
+            fetch_zp(h, EXPERT_PAIRS[0])
+            fetch_codes(h, second, HIGH)
+            fetch_zp(h, EXPERT_PAIRS[1])
+            fetch_codes(h, third, HIGH)
 
         identity = held.tile([P, P], BF16, name="identity")
         masks.make_identity(nc, identity[:])

@@ -9,14 +9,13 @@ E, K, C, S, N = 4, 1024, 1024, 2048, 1024
 R = K // P
 H = N // E
 BLOCKS = C // P
-HALF = C // 2
-HALVES = C // HALF
-RH = R // 2
-LOW, HIGH = slice(0, RH), slice(RH, R)
-BANK = 2 * H
+BANK = 512
+BANKS_OF_SCALES = C // BANK
 GPSIMD_EXPERT = 0
-VECTOR_EXPERTS = [e for e in range(E) if e != GPSIMD_EXPERT]
-EXPERT_PAIRS = (slice(0, 2), slice(2, 4))
+VECTOR_EXPERTS = (1, 2, 3)
+HALVES = (slice(0, R // 2), slice(R // 2, R))
+LOW_QUARTERS = (slice(0, R // 4), slice(R // 4, R // 2))
+HIGH_QUARTERS = (slice(R // 2, 3 * R // 4), slice(3 * R // 4, R))
 SUMS_AHEAD = 4
 
 FLOPS = 2 * C * N * (K + P)
@@ -26,34 +25,43 @@ def tile_moewna16matmul_b_kernel(tc, base, state, q, scale, zp, offs, out):
     nc = tc.nc
     q_view = q.rearrange("e (r u) c -> e u r c", u=P)
     state_view = state.rearrange("(r u) j -> u r j", u=P)
-    scale_view = scale.rearrange("e u c -> u e c")
-    zp_view = zp.rearrange("e u c -> u e c")
 
     with (
         tc.tile_pool(name="held", bufs=1) as held,
         tc.tile_pool(name="streamed", bufs=BLOCKS) as streamed,
         tc.tile_pool(name="sums", bufs=SUMS_AHEAD) as sums_pool,
-        tc.psum_pool(name="scale_psum", bufs=4) as scale_psum,
+        tc.psum_pool(name="scale_psum", bufs=2 * BANKS_OF_SCALES) as scale_psum,
         tc.psum_pool(name="psum", bufs=2) as psum,
     ):
         offsets = held.tile([P, N // 16], U16, name="offsets")
         nc.sync.dma_start(offsets[:], offs)
 
         tokens = held.tile([P, R, N], BF16, name="tokens")
-        scales = [held.tile([P, E, HALF], F32, name=f"scales{h}") for h in range(HALVES)]
-        minus_scales = [held.tile([P, E, HALF], F32, name=f"minus_scales{h}") for h in range(HALVES)]
-        zero_points = [held.tile([P, E, HALF], F32, name=f"zero_points{h}") for h in range(HALVES)]
-        w = [held.tile([P, E, R, HALF], BF16, name=f"w{h}") for h in range(HALVES)]
-        nz = [held.tile([P, E, HALF], BF16, name=f"nz{h}") for h in range(HALVES)]
-        codes = [
-            [streamed.tile([P, R, HALF], BF16, name="codes", tag="streamed") for e in range(E)] for h in range(HALVES)
+        scales = [held.tile([P, 1, C], F32, name=f"scales{e}") for e in range(E)]
+        minus_scales = [held.tile([P, C], F32, name=f"minus_scales{e}") for e in range(E)]
+        zero_points = [held.tile([P, C], F32, name=f"zero_points{e}") for e in range(E)]
+        w = [
+            [held.tile([P, R, BANK], BF16, name=f"w{e}_{k}") for k in range(BANKS_OF_SCALES)] for e in range(E)
         ]
+        nz = [held.tile([P, C], BF16, name=f"nz{e}") for e in range(E)]
+        codes = {}
+        for e in (VECTOR_EXPERTS[0], GPSIMD_EXPERT) + VECTOR_EXPERTS[1:]:
+            codes[e] = [streamed.tile([P, R // 2, C], BF16, name="codes", tag="streamed") for half in HALVES]
 
-        def fetch_codes(h, e, rows):
-            nc.sync.dma_start(codes[h][e][:, rows, :], q_view[e, :, rows, h * HALF : (h + 1) * HALF])
+        def codes_of(e, rows):
+            half = rows.start // (R // 2)
+            first_row = half * (R // 2)
+            return codes[e][half][:, rows.start - first_row : rows.stop - first_row, :]
 
-        def fetch_zp(h, pair):
-            nc.sync.dma_start(zero_points[h][:, pair, :], zp_view[:, pair, h * HALF : (h + 1) * HALF])
+        def fetch_scales(e):
+            nc.sync.dma_start(scales[e][:, 0, :], scale[e])
+            nc.scalar.mul(minus_scales[e][:], scales[e][:, 0, :], -1.0)
+
+        def fetch_codes(e, rows):
+            nc.sync.dma_start(codes_of(e, rows), q_view[e, :, rows, :])
+
+        def fetch_zp(e):
+            nc.sync.dma_start(zero_points[e][:], zp[e])
 
         def fetch_tokens(bank):
             columns = slice(bank * BANK, (bank + 1) * BANK)
@@ -64,33 +72,42 @@ def tile_moewna16matmul_b_kernel(tc, base, state, q, scale, zp, offs, out):
             nc.sync.dma_start(window[:], base[b * P : (b + 1) * P, :])
             return window
 
-        def scale_to_psum(h, e):
-            scale_ps = scale_psum.tile([P, 1, HALF], F32, name="scale_ps")
-            nc.tensor.matmul(scale_ps[:, 0, :], identity32[:], scales[h][:, e, :], start=True, stop=True)
-            return scale_ps
+        def scales_to_psum(e):
+            banks = []
+            for k in range(BANKS_OF_SCALES):
+                scale_ps = scale_psum.tile([P, 1, BANK], F32, name="scale_ps")
+                nc.tensor.matmul(
+                    scale_ps[:, 0, :], identity32[:], scales[e][:, 0, k * BANK : (k + 1) * BANK], start=True, stop=True
+                )
+                banks.append(scale_ps)
+            return banks
 
-        def dequantize(h, scale_ps_of_expert):
-            nc.scalar.mul(minus_scales[h][:], scales[h][:], -1.0)
-            for rows in (LOW, HIGH):
-                nc.gpsimd.tensor_tensor(
-                    w[h][:, GPSIMD_EXPERT, rows, :],
-                    codes[h][GPSIMD_EXPERT][:, rows, :],
-                    scales[h][:, GPSIMD_EXPERT : GPSIMD_EXPERT + 1, :].to_broadcast([P, RH, HALF]),
+        def multiply_on_vector(e, rows, scale_banks):
+            for k, scale_ps in enumerate(scale_banks):
+                columns = slice(k * BANK, (k + 1) * BANK)
+                nc.vector.tensor_tensor(
+                    w[e][k][:, rows, :],
+                    codes_of(e, rows)[:, :, columns],
+                    scale_ps[:].to_broadcast([P, rows.stop - rows.start, BANK]),
                     MULT,
                 )
-                for e in VECTOR_EXPERTS:
-                    nc.vector.tensor_tensor(
-                        w[h][:, e, rows, :],
-                        codes[h][e][:, rows, :],
-                        scale_ps_of_expert[e][:].to_broadcast([P, RH, HALF]),
-                        MULT,
-                    )
-            for pair in EXPERT_PAIRS:
-                nc.gpsimd.tensor_tensor(nz[h][:, pair, :], zero_points[h][:, pair, :], minus_scales[h][:, pair, :], MULT)
 
-        def multiply(b):
-            h = b * P // HALF
-            columns = slice(b * P - h * HALF, (b + 1) * P - h * HALF)
+        def multiply_on_gpsimd(rows, k):
+            columns = slice(k * BANK, (k + 1) * BANK)
+            nc.gpsimd.tensor_tensor(
+                w[GPSIMD_EXPERT][k][:, rows, :],
+                codes_of(GPSIMD_EXPERT, rows)[:, :, columns],
+                scales[GPSIMD_EXPERT][:, :, columns].to_broadcast([P, rows.stop - rows.start, BANK]),
+                MULT,
+            )
+
+        def nz_on_gpsimd(e):
+            nc.gpsimd.tensor_tensor(nz[e][:], zero_points[e][:], minus_scales[e][:], MULT)
+
+        def sums_of_block(b):
+            columns = slice(b * P, (b + 1) * P)
+            k = b * P // BANK
+            columns_of_w = slice(b * P - k * BANK, (b + 1) * P - k * BANK)
             main = sums_pool.tile([P, N], F32, name="main")
             corr = sums_pool.tile([P, N], F32, name="corr")
             for bank in range(N // BANK):
@@ -99,7 +116,7 @@ def tile_moewna16matmul_b_kernel(tc, base, state, q, scale, zp, offs, out):
                     for r in range(R):
                         nc.tensor.matmul(
                             main_ps[:, (e % 2) * H : (e % 2 + 1) * H],
-                            w[h][:, e, r, columns],
+                            w[e][k][:, r, columns_of_w],
                             tokens[:, r, e * H : (e + 1) * H],
                             start=(r == 0),
                             stop=(r == R - 1),
@@ -110,7 +127,7 @@ def tile_moewna16matmul_b_kernel(tc, base, state, q, scale, zp, offs, out):
                 for e in (2 * bank, 2 * bank + 1):
                     nc.tensor.matmul(
                         corr_ps[:, (e % 2) * H : (e % 2 + 1) * H],
-                        nz[h][:, e, columns],
+                        nz[e][:, columns],
                         xs[:, e * H : (e + 1) * H],
                         start=True,
                         stop=True,
@@ -118,37 +135,51 @@ def tile_moewna16matmul_b_kernel(tc, base, state, q, scale, zp, offs, out):
                 nc.scalar.copy(corr[:, bank * BANK : (bank + 1) * BANK], corr_ps[:])
             return main, corr
 
-        for h in range(HALVES):
-            first, second, third = VECTOR_EXPERTS
-            nc.sync.dma_start(scales[h][:], scale_view[:, :, h * HALF : (h + 1) * HALF])
-            fetch_codes(h, GPSIMD_EXPERT, LOW)
-            fetch_codes(h, first, LOW)
-            fetch_codes(h, second, LOW)
-            if h == HALVES - 1:
-                fetch_tokens(0)
-            fetch_codes(h, GPSIMD_EXPERT, HIGH)
-            fetch_codes(h, third, LOW)
-            if h == HALVES - 1:
-                fetch_tokens(1)
-            fetch_codes(h, first, HIGH)
-            fetch_zp(h, EXPERT_PAIRS[0])
-            fetch_codes(h, second, HIGH)
-            fetch_zp(h, EXPERT_PAIRS[1])
-            fetch_codes(h, third, HIGH)
+        first, second, third = VECTOR_EXPERTS
+        low, high = HALVES
+        fetch_scales(first)
+        fetch_codes(first, LOW_QUARTERS[0])
+        fetch_scales(GPSIMD_EXPERT)
+        fetch_codes(GPSIMD_EXPERT, LOW_QUARTERS[0])
+        fetch_codes(first, LOW_QUARTERS[1])
+        fetch_codes(first, high)
+        fetch_codes(GPSIMD_EXPERT, LOW_QUARTERS[1])
+        fetch_scales(second)
+        fetch_codes(second, low)
+        fetch_zp(0)
+        fetch_zp(1)
+        fetch_codes(second, high)
+        fetch_codes(GPSIMD_EXPERT, high)
+        fetch_tokens(0)
+        fetch_scales(third)
+        fetch_zp(2)
+        fetch_codes(third, low)
+        fetch_tokens(1)
+        fetch_zp(3)
+        fetch_codes(third, HIGH_QUARTERS[0])
+        fetch_codes(third, HIGH_QUARTERS[1])
 
-        identity = held.tile([P, P], BF16, name="identity")
-        masks.make_identity(nc, identity[:])
         identity32 = held.tile([P, P], F32, name="identity32")
         masks.make_identity(nc, identity32[:])
+        identity = held.tile([P, P], BF16, name="identity")
+        masks.make_identity(nc, identity[:])
 
-        scale_ps = {h: {} for h in range(HALVES)}
-        for e in VECTOR_EXPERTS:
-            scale_ps[0][e] = scale_to_psum(0, e)
-        for h in range(HALVES):
-            dequantize(h, scale_ps[h])
-            if h + 1 < HALVES:
-                for e in VECTOR_EXPERTS:
-                    scale_ps[h + 1][e] = scale_to_psum(h + 1, e)
+        scale_banks = {e: scales_to_psum(e) for e in VECTOR_EXPERTS}
+        for rows in LOW_QUARTERS + (high,):
+            multiply_on_vector(first, rows, scale_banks[first])
+        for rows in HALVES:
+            multiply_on_vector(second, rows, scale_banks[second])
+        for rows in (low,) + HIGH_QUARTERS:
+            multiply_on_vector(third, rows, scale_banks[third])
+        for rows in LOW_QUARTERS:
+            multiply_on_gpsimd(rows, 0)
+            multiply_on_gpsimd(rows, 1)
+        nz_on_gpsimd(0)
+        nz_on_gpsimd(1)
+        multiply_on_gpsimd(high, 0)
+        nz_on_gpsimd(2)
+        nz_on_gpsimd(3)
+        multiply_on_gpsimd(high, 1)
 
         xs = held.tile([P, N], BF16, name="xs")
         for bank in range(N // BANK):
@@ -163,7 +194,7 @@ def tile_moewna16matmul_b_kernel(tc, base, state, q, scale, zp, offs, out):
                 )
             nc.scalar.copy(xs[:, bank * BANK : (bank + 1) * BANK], xs_ps[:])
 
-        sums = {b: multiply(b) for b in range(SUMS_AHEAD)}
+        sums = {b: sums_of_block(b) for b in range(SUMS_AHEAD)}
 
         windows = [fetch_window(b) for b in range(BLOCKS)]
         for b in range(BLOCKS):
@@ -171,4 +202,4 @@ def tile_moewna16matmul_b_kernel(tc, base, state, q, scale, zp, offs, out):
             nc.vector.tensor_tensor(windows[b][:].indirect(offsets[:]), main[:], corr[:], ADD)
             nc.sync.dma_start(out[b * P : (b + 1) * P, :], windows[b][:])
             if b + SUMS_AHEAD < BLOCKS:
-                sums[b + SUMS_AHEAD] = multiply(b + SUMS_AHEAD)
+                sums[b + SUMS_AHEAD] = sums_of_block(b + SUMS_AHEAD)

@@ -11,11 +11,12 @@ H = N // E
 BLOCKS = C // P
 BANK = 512
 BANKS_OF_SCALES = C // BANK
-GPSIMD_EXPERT = 0
-VECTOR_EXPERTS = (1, 2, 3)
+GPSIMD_EXPERT = 3
+VECTOR_EXPERTS = (0, 1, 2)
 HALVES = (slice(0, R // 2), slice(R // 2, R))
 LOW_QUARTERS = (slice(0, R // 4), slice(R // 4, R // 2))
-HIGH_QUARTERS = (slice(R // 2, 3 * R // 4), slice(3 * R // 4, R))
+ALL_COLUMNS = slice(0, C)
+COLUMNS = tuple(slice(k * BANK, (k + 1) * BANK) for k in range(C // BANK))
 SUMS_AHEAD = 4
 
 FLOPS = 2 * C * N * (K + P)
@@ -57,8 +58,8 @@ def tile_moewna16matmul_b_kernel(tc, base, state, q, scale, zp, offs, out):
             nc.sync.dma_start(scales[e][:, 0, :], scale[e])
             nc.scalar.mul(minus_scales[e][:], scales[e][:, 0, :], -1.0)
 
-        def fetch_codes(e, rows):
-            nc.sync.dma_start(codes_of(e, rows), q_view[e, :, rows, :])
+        def fetch_codes(e, rows, columns=ALL_COLUMNS):
+            nc.sync.dma_start(codes_of(e, rows)[:, :, columns], q_view[e, :, rows, columns])
 
         def fetch_zp(e):
             nc.sync.dma_start(zero_points[e][:], zp[e])
@@ -82,18 +83,16 @@ def tile_moewna16matmul_b_kernel(tc, base, state, q, scale, zp, offs, out):
                 banks.append(scale_ps)
             return banks
 
-        def multiply_on_vector(e, rows, scale_banks):
-            for k, scale_ps in enumerate(scale_banks):
-                columns = slice(k * BANK, (k + 1) * BANK)
-                nc.vector.tensor_tensor(
-                    w[e][k][:, rows, :],
-                    codes_of(e, rows)[:, :, columns],
-                    scale_ps[:].to_broadcast([P, rows.stop - rows.start, BANK]),
-                    MULT,
-                )
+        def multiply_on_vector(e, rows, k):
+            nc.vector.tensor_tensor(
+                w[e][k][:, rows, :],
+                codes_of(e, rows)[:, :, COLUMNS[k]],
+                scale_banks[e][k][:].to_broadcast([P, rows.stop - rows.start, BANK]),
+                MULT,
+            )
 
         def multiply_on_gpsimd(rows, k):
-            columns = slice(k * BANK, (k + 1) * BANK)
+            columns = COLUMNS[k]
             nc.gpsimd.tensor_tensor(
                 w[GPSIMD_EXPERT][k][:, rows, :],
                 codes_of(GPSIMD_EXPERT, rows)[:, :, columns],
@@ -146,18 +145,21 @@ def tile_moewna16matmul_b_kernel(tc, base, state, q, scale, zp, offs, out):
         fetch_codes(GPSIMD_EXPERT, LOW_QUARTERS[1])
         fetch_scales(second)
         fetch_codes(second, low)
-        fetch_zp(0)
-        fetch_zp(1)
-        fetch_codes(second, high)
-        fetch_codes(GPSIMD_EXPERT, high)
+        fetch_zp(first)
+        fetch_zp(second)
+        fetch_codes(second, high, COLUMNS[0])
+        fetch_zp(GPSIMD_EXPERT)
         fetch_tokens(0)
         fetch_scales(third)
-        fetch_zp(2)
-        fetch_codes(third, low)
+        fetch_zp(third)
+        fetch_codes(second, high, COLUMNS[1])
+        fetch_codes(GPSIMD_EXPERT, high, COLUMNS[0])
+        fetch_codes(third, low, COLUMNS[0])
         fetch_tokens(1)
-        fetch_zp(3)
-        fetch_codes(third, HIGH_QUARTERS[0])
-        fetch_codes(third, HIGH_QUARTERS[1])
+        fetch_codes(third, high, COLUMNS[0])
+        fetch_codes(GPSIMD_EXPERT, high, COLUMNS[1])
+        fetch_codes(third, low, COLUMNS[1])
+        fetch_codes(third, high, COLUMNS[1])
 
         identity32 = held.tile([P, P], F32, name="identity32")
         masks.make_identity(nc, identity32[:])
@@ -166,19 +168,20 @@ def tile_moewna16matmul_b_kernel(tc, base, state, q, scale, zp, offs, out):
 
         scale_banks = {e: scales_to_psum(e) for e in VECTOR_EXPERTS}
         for rows in LOW_QUARTERS + (high,):
-            multiply_on_vector(first, rows, scale_banks[first])
+            for k in range(BANKS_OF_SCALES):
+                multiply_on_vector(first, rows, k)
         for rows in HALVES:
-            multiply_on_vector(second, rows, scale_banks[second])
-        for rows in (low,) + HIGH_QUARTERS:
-            multiply_on_vector(third, rows, scale_banks[third])
+            for k in range(BANKS_OF_SCALES):
+                multiply_on_vector(second, rows, k)
+        for k in range(BANKS_OF_SCALES):
+            for rows in HALVES:
+                multiply_on_vector(third, rows, k)
         for rows in LOW_QUARTERS:
             multiply_on_gpsimd(rows, 0)
             multiply_on_gpsimd(rows, 1)
-        nz_on_gpsimd(0)
-        nz_on_gpsimd(1)
+        for e in (first, second, GPSIMD_EXPERT, third):
+            nz_on_gpsimd(e)
         multiply_on_gpsimd(high, 0)
-        nz_on_gpsimd(2)
-        nz_on_gpsimd(3)
         multiply_on_gpsimd(high, 1)
 
         xs = held.tile([P, N], BF16, name="xs")

@@ -14,7 +14,6 @@ BANKS_OF_SCALES = C // BANK
 GPSIMD_EXPERT = 3
 VECTOR_EXPERTS = (0, 1, 2)
 HALVES = (slice(0, R // 2), slice(R // 2, R))
-LOW_QUARTERS = (slice(0, R // 4), slice(R // 4, R // 2))
 ALL_COLUMNS = slice(0, C)
 COLUMNS = tuple(slice(k * BANK, (k + 1) * BANK) for k in range(C // BANK))
 SUMS_AHEAD = 4
@@ -22,10 +21,16 @@ SUMS_AHEAD = 4
 FLOPS = 2 * C * N * (K + P)
 
 
+def only(e):
+    return slice(e, e + 1)
+
+
 def tile_moewna16matmul_b_kernel(tc, base, state, q, scale, zp, offs, out):
     nc = tc.nc
     q_view = q.rearrange("e (r u) c -> e u r c", u=P)
     state_view = state.rearrange("(r u) j -> u r j", u=P)
+    scale_view = scale.rearrange("e u c -> u e c")
+    zp_view = zp.rearrange("e u c -> u e c")
 
     with (
         tc.tile_pool(name="held", bufs=1) as held,
@@ -38,15 +43,15 @@ def tile_moewna16matmul_b_kernel(tc, base, state, q, scale, zp, offs, out):
         nc.sync.dma_start(offsets[:], offs)
 
         tokens = held.tile([P, R, N], BF16, name="tokens")
-        scales = [held.tile([P, 1, C], F32, name=f"scales{e}") for e in range(E)]
-        minus_scales = [held.tile([P, C], F32, name=f"minus_scales{e}") for e in range(E)]
-        zero_points = [held.tile([P, C], F32, name=f"zero_points{e}") for e in range(E)]
+        scales = held.tile([P, E, C], F32, name="scales")
+        minus_scales = held.tile([P, E, C], F32, name="minus_scales")
+        zero_points = held.tile([P, E, C], F32, name="zero_points")
         w = [
             [held.tile([P, R, BANK], BF16, name=f"w{e}_{k}") for k in range(BANKS_OF_SCALES)] for e in range(E)
         ]
-        nz = [held.tile([P, C], BF16, name=f"nz{e}") for e in range(E)]
+        nz = held.tile([P, E, C], BF16, name="nz")
         codes = {}
-        for e in (VECTOR_EXPERTS[0], GPSIMD_EXPERT) + VECTOR_EXPERTS[1:]:
+        for e in (GPSIMD_EXPERT,) + VECTOR_EXPERTS:
             codes[e] = [streamed.tile([P, R // 2, C], BF16, name="codes", tag="streamed") for half in HALVES]
 
         def codes_of(e, rows):
@@ -54,15 +59,15 @@ def tile_moewna16matmul_b_kernel(tc, base, state, q, scale, zp, offs, out):
             first_row = half * (R // 2)
             return codes[e][half][:, rows.start - first_row : rows.stop - first_row, :]
 
-        def fetch_scales(e):
-            nc.sync.dma_start(scales[e][:, 0, :], scale[e])
-            nc.scalar.mul(minus_scales[e][:], scales[e][:, 0, :], -1.0)
+        def fetch_scales(experts):
+            nc.sync.dma_start(scales[:, experts, :], scale_view[:, experts, :])
+            nc.scalar.mul(minus_scales[:, experts, :], scales[:, experts, :], -1.0)
 
         def fetch_codes(e, rows, columns=ALL_COLUMNS):
             nc.sync.dma_start(codes_of(e, rows)[:, :, columns], q_view[e, :, rows, columns])
 
-        def fetch_zp(e):
-            nc.sync.dma_start(zero_points[e][:], zp[e])
+        def fetch_zp(experts):
+            nc.sync.dma_start(zero_points[:, experts, :], zp_view[:, experts, :])
 
         def fetch_tokens(bank):
             columns = slice(bank * BANK, (bank + 1) * BANK)
@@ -78,7 +83,7 @@ def tile_moewna16matmul_b_kernel(tc, base, state, q, scale, zp, offs, out):
             for k in range(BANKS_OF_SCALES):
                 scale_ps = scale_psum.tile([P, 1, BANK], F32, name="scale_ps")
                 nc.tensor.matmul(
-                    scale_ps[:, 0, :], identity32[:], scales[e][:, 0, k * BANK : (k + 1) * BANK], start=True, stop=True
+                    scale_ps[:, 0, :], identity32[:], scales[:, e, k * BANK : (k + 1) * BANK], start=True, stop=True
                 )
                 banks.append(scale_ps)
             return banks
@@ -96,12 +101,12 @@ def tile_moewna16matmul_b_kernel(tc, base, state, q, scale, zp, offs, out):
             nc.gpsimd.tensor_tensor(
                 w[GPSIMD_EXPERT][k][:, rows, :],
                 codes_of(GPSIMD_EXPERT, rows)[:, :, columns],
-                scales[GPSIMD_EXPERT][:, :, columns].to_broadcast([P, rows.stop - rows.start, BANK]),
+                scales[:, only(GPSIMD_EXPERT), columns].to_broadcast([P, rows.stop - rows.start, BANK]),
                 MULT,
             )
 
-        def nz_on_gpsimd(e):
-            nc.gpsimd.tensor_tensor(nz[e][:], zero_points[e][:], minus_scales[e][:], MULT)
+        def nz_on_gpsimd(experts):
+            nc.gpsimd.tensor_tensor(nz[:, experts, :], zero_points[:, experts, :], minus_scales[:, experts, :], MULT)
 
         def sums_of_block(b):
             columns = slice(b * P, (b + 1) * P)
@@ -126,7 +131,7 @@ def tile_moewna16matmul_b_kernel(tc, base, state, q, scale, zp, offs, out):
                 for e in (2 * bank, 2 * bank + 1):
                     nc.tensor.matmul(
                         corr_ps[:, (e % 2) * H : (e % 2 + 1) * H],
-                        nz[e][:, columns],
+                        nz[:, e, columns],
                         xs[:, e * H : (e + 1) * H],
                         start=True,
                         stop=True,
@@ -136,22 +141,19 @@ def tile_moewna16matmul_b_kernel(tc, base, state, q, scale, zp, offs, out):
 
         first, second, third = VECTOR_EXPERTS
         low, high = HALVES
-        fetch_scales(first)
-        fetch_codes(first, LOW_QUARTERS[0])
-        fetch_scales(GPSIMD_EXPERT)
-        fetch_codes(GPSIMD_EXPERT, LOW_QUARTERS[0])
-        fetch_codes(first, LOW_QUARTERS[1])
+        both_early = slice(first, second + 1)
+        fetch_scales(only(GPSIMD_EXPERT))
+        fetch_codes(GPSIMD_EXPERT, low)
+        fetch_scales(both_early)
+        fetch_codes(first, low)
         fetch_codes(first, high)
-        fetch_codes(GPSIMD_EXPERT, LOW_QUARTERS[1])
-        fetch_scales(second)
         fetch_codes(second, low)
-        fetch_zp(first)
-        fetch_zp(second)
+        fetch_zp(both_early)
         fetch_codes(second, high, COLUMNS[0])
-        fetch_zp(GPSIMD_EXPERT)
+        fetch_zp(only(GPSIMD_EXPERT))
         fetch_tokens(0)
-        fetch_scales(third)
-        fetch_zp(third)
+        fetch_scales(only(third))
+        fetch_zp(only(third))
         fetch_codes(second, high, COLUMNS[1])
         fetch_codes(GPSIMD_EXPERT, high, COLUMNS[0])
         fetch_codes(third, low, COLUMNS[0])
@@ -167,20 +169,17 @@ def tile_moewna16matmul_b_kernel(tc, base, state, q, scale, zp, offs, out):
         masks.make_identity(nc, identity[:])
 
         scale_banks = {e: scales_to_psum(e) for e in VECTOR_EXPERTS}
-        for rows in LOW_QUARTERS + (high,):
-            for k in range(BANKS_OF_SCALES):
-                multiply_on_vector(first, rows, k)
-        for rows in HALVES:
-            for k in range(BANKS_OF_SCALES):
-                multiply_on_vector(second, rows, k)
+        for e in (first, second):
+            for rows in HALVES:
+                for k in range(BANKS_OF_SCALES):
+                    multiply_on_vector(e, rows, k)
         for k in range(BANKS_OF_SCALES):
             for rows in HALVES:
                 multiply_on_vector(third, rows, k)
-        for rows in LOW_QUARTERS:
-            multiply_on_gpsimd(rows, 0)
-            multiply_on_gpsimd(rows, 1)
-        for e in (first, second, GPSIMD_EXPERT, third):
-            nz_on_gpsimd(e)
+        multiply_on_gpsimd(low, 0)
+        multiply_on_gpsimd(low, 1)
+        for experts in (both_early, only(GPSIMD_EXPERT), only(third)):
+            nz_on_gpsimd(experts)
         multiply_on_gpsimd(high, 0)
         multiply_on_gpsimd(high, 1)
 

@@ -11,18 +11,16 @@ H = N // E
 BLOCKS = C // P
 BANK = 512
 BANKS_OF_SCALES = C // BANK
-GPSIMD_EXPERT = 3
-VECTOR_EXPERTS = (0, 1, 2)
-HALVES = (slice(0, R // 2), slice(R // 2, R))
+GPSIMD_EXPERT = 2
+FIRST, SECOND, LAST = VECTOR_EXPERTS = (0, 1, 3)
+ALL_BUT_LAST, ONLY_LAST = slice(0, LAST), slice(LAST, E)
+ALL_ROWS, LOW, HIGH = slice(0, R), slice(0, R // 2), slice(R // 2, R)
 ALL_COLUMNS = slice(0, C)
-COLUMNS = tuple(slice(k * BANK, (k + 1) * BANK) for k in range(C // BANK))
+LOWER, UPPER = slice(0, BANK), slice(BANK, C)
+COLUMNS = (LOWER, UPPER)
 SUMS_AHEAD = 4
 
 FLOPS = 2 * C * N * (K + P)
-
-
-def only(e):
-    return slice(e, e + 1)
 
 
 def tile_moewna16matmul_b_kernel(tc, base, state, q, scale, zp, offs, out):
@@ -51,20 +49,20 @@ def tile_moewna16matmul_b_kernel(tc, base, state, q, scale, zp, offs, out):
         ]
         nz = held.tile([P, E, C], BF16, name="nz")
         codes = {}
-        for e in (GPSIMD_EXPERT,) + VECTOR_EXPERTS:
-            codes[e] = [streamed.tile([P, R // 2, C], BF16, name="codes", tag="streamed") for half in HALVES]
-
-        def codes_of(e, rows):
-            half = rows.start // (R // 2)
-            first_row = half * (R // 2)
-            return codes[e][half][:, rows.start - first_row : rows.stop - first_row, :]
+        for e in (GPSIMD_EXPERT, FIRST, SECOND):
+            for rows in (LOW, HIGH):
+                codes[e, rows.start] = streamed.tile([P, R // 2, C], BF16, name="codes", tag="streamed")
+        last_codes = [streamed.tile([P, R, BANK], BF16, name="last_codes", tag="streamed") for k in range(2)]
 
         def fetch_scales(experts):
             nc.sync.dma_start(scales[:, experts, :], scale_view[:, experts, :])
             nc.scalar.mul(minus_scales[:, experts, :], scales[:, experts, :], -1.0)
 
         def fetch_codes(e, rows, columns=ALL_COLUMNS):
-            nc.sync.dma_start(codes_of(e, rows)[:, :, columns], q_view[e, :, rows, columns])
+            nc.sync.dma_start(codes[e, rows.start][:, :, columns], q_view[e, :, rows, columns])
+
+        def fetch_last_codes(k, rows):
+            nc.sync.dma_start(last_codes[k][:, rows, :], q_view[LAST, :, rows, COLUMNS[k]])
 
         def fetch_zp(experts):
             nc.sync.dma_start(zero_points[:, experts, :], zp_view[:, experts, :])
@@ -88,20 +86,19 @@ def tile_moewna16matmul_b_kernel(tc, base, state, q, scale, zp, offs, out):
                 banks.append(scale_ps)
             return banks
 
-        def multiply_on_vector(e, rows, k):
+        def multiply_on_vector(e, k, rows, tile):
             nc.vector.tensor_tensor(
                 w[e][k][:, rows, :],
-                codes_of(e, rows)[:, :, COLUMNS[k]],
+                tile,
                 scale_banks[e][k][:].to_broadcast([P, rows.stop - rows.start, BANK]),
                 MULT,
             )
 
-        def multiply_on_gpsimd(rows, k):
-            columns = COLUMNS[k]
+        def multiply_on_gpsimd(k, rows):
             nc.gpsimd.tensor_tensor(
                 w[GPSIMD_EXPERT][k][:, rows, :],
-                codes_of(GPSIMD_EXPERT, rows)[:, :, columns],
-                scales[:, only(GPSIMD_EXPERT), columns].to_broadcast([P, rows.stop - rows.start, BANK]),
+                codes[GPSIMD_EXPERT, rows.start][:, :, COLUMNS[k]],
+                scales[:, GPSIMD_EXPERT : GPSIMD_EXPERT + 1, COLUMNS[k]].to_broadcast([P, R // 2, BANK]),
                 MULT,
             )
 
@@ -139,29 +136,22 @@ def tile_moewna16matmul_b_kernel(tc, base, state, q, scale, zp, offs, out):
                 nc.scalar.copy(corr[:, bank * BANK : (bank + 1) * BANK], corr_ps[:])
             return main, corr
 
-        first, second, third = VECTOR_EXPERTS
-        low, high = HALVES
-        both_early = slice(first, second + 1)
-        fetch_scales(only(GPSIMD_EXPERT))
-        fetch_codes(GPSIMD_EXPERT, low)
-        fetch_scales(both_early)
-        fetch_codes(first, low)
-        fetch_codes(first, high)
-        fetch_codes(second, low)
-        fetch_zp(both_early)
-        fetch_codes(second, high, COLUMNS[0])
-        fetch_zp(only(GPSIMD_EXPERT))
+        fetch_scales(ALL_BUT_LAST)
+        fetch_codes(GPSIMD_EXPERT, LOW)
+        fetch_codes(FIRST, LOW)
+        fetch_codes(FIRST, HIGH)
+        fetch_zp(ALL_BUT_LAST)
+        fetch_codes(SECOND, LOW)
+        fetch_codes(SECOND, HIGH)
         fetch_tokens(0)
-        fetch_scales(only(third))
-        fetch_zp(only(third))
-        fetch_codes(second, high, COLUMNS[1])
-        fetch_codes(GPSIMD_EXPERT, high, COLUMNS[0])
-        fetch_codes(third, low, COLUMNS[0])
+        fetch_scales(ONLY_LAST)
+        fetch_zp(ONLY_LAST)
+        fetch_codes(GPSIMD_EXPERT, HIGH, LOWER)
+        fetch_last_codes(0, ALL_ROWS)
         fetch_tokens(1)
-        fetch_codes(third, high, COLUMNS[0])
-        fetch_codes(GPSIMD_EXPERT, high, COLUMNS[1])
-        fetch_codes(third, low, COLUMNS[1])
-        fetch_codes(third, high, COLUMNS[1])
+        fetch_codes(GPSIMD_EXPERT, HIGH, UPPER)
+        fetch_last_codes(1, LOW)
+        fetch_last_codes(1, HIGH)
 
         identity32 = held.tile([P, P], F32, name="identity32")
         masks.make_identity(nc, identity32[:])
@@ -169,19 +159,19 @@ def tile_moewna16matmul_b_kernel(tc, base, state, q, scale, zp, offs, out):
         masks.make_identity(nc, identity[:])
 
         scale_banks = {e: scales_to_psum(e) for e in VECTOR_EXPERTS}
-        for e in (first, second):
-            for rows in HALVES:
+        for e in (FIRST, SECOND):
+            for rows in (LOW, HIGH):
                 for k in range(BANKS_OF_SCALES):
-                    multiply_on_vector(e, rows, k)
+                    multiply_on_vector(e, k, rows, codes[e, rows.start][:, :, COLUMNS[k]])
+        multiply_on_vector(LAST, 0, ALL_ROWS, last_codes[0][:])
+        for rows in (LOW, HIGH):
+            multiply_on_vector(LAST, 1, rows, last_codes[1][:, rows, :])
         for k in range(BANKS_OF_SCALES):
-            for rows in HALVES:
-                multiply_on_vector(third, rows, k)
-        multiply_on_gpsimd(low, 0)
-        multiply_on_gpsimd(low, 1)
-        for experts in (both_early, only(GPSIMD_EXPERT), only(third)):
-            nz_on_gpsimd(experts)
-        multiply_on_gpsimd(high, 0)
-        multiply_on_gpsimd(high, 1)
+            multiply_on_gpsimd(k, LOW)
+        nz_on_gpsimd(ALL_BUT_LAST)
+        nz_on_gpsimd(ONLY_LAST)
+        for k in range(BANKS_OF_SCALES):
+            multiply_on_gpsimd(k, HIGH)
 
         xs = held.tile([P, N], BF16, name="xs")
         for bank in range(N // BANK):

@@ -15,6 +15,7 @@ GPSIMD_EXPERT = 2
 FIRST, SECOND, LAST = VECTOR_EXPERTS = (0, 1, 3)
 ALL_BUT_LAST, ONLY_LAST = slice(0, LAST), slice(LAST, E)
 ALL_ROWS, LOW, HIGH = slice(0, R), slice(0, R // 2), slice(R // 2, R)
+QUARTERS = (slice(0, R // 4), slice(R // 4, R // 2))
 ALL_COLUMNS = slice(0, C)
 LOWER, UPPER = slice(0, BANK), slice(BANK, C)
 COLUMNS = (LOWER, UPPER)
@@ -38,8 +39,6 @@ def tile_moewna16matmul_b_kernel(tc, base, state, q, scale, zp, offs, out):
         tc.psum_pool(name="psum", bufs=2) as psum,
     ):
         offsets = held.tile([P, N // 16], U16, name="offsets")
-        nc.sync.dma_start(offsets[:], offs)
-
         tokens = held.tile([P, R, N], BF16, name="tokens")
         scales = held.tile([P, E, C], F32, name="scales")
         minus_scales = held.tile([P, E, C], F32, name="minus_scales")
@@ -51,15 +50,19 @@ def tile_moewna16matmul_b_kernel(tc, base, state, q, scale, zp, offs, out):
         codes = {}
         for e in (GPSIMD_EXPERT, FIRST, SECOND):
             for rows in (LOW, HIGH):
-                codes[e, rows.start] = streamed.tile([P, R // 2, C], BF16, name="codes", tag="streamed")
+                codes[e, rows.start // LOW.stop] = streamed.tile([P, R // 2, C], BF16, name="codes", tag="streamed")
         last_codes = [streamed.tile([P, R, BANK], BF16, name="last_codes", tag="streamed") for k in range(2)]
 
         def fetch_scales(experts):
             nc.sync.dma_start(scales[:, experts, :], scale_view[:, experts, :])
             nc.scalar.mul(minus_scales[:, experts, :], scales[:, experts, :], -1.0)
 
+        def codes_of(e, rows):
+            half = rows.start // LOW.stop
+            return codes[e, half][:, rows.start - half * LOW.stop : rows.stop - half * LOW.stop, :]
+
         def fetch_codes(e, rows, columns=ALL_COLUMNS):
-            nc.sync.dma_start(codes[e, rows.start][:, :, columns], q_view[e, :, rows, columns])
+            nc.sync.dma_start(codes_of(e, rows)[:, :, columns], q_view[e, :, rows, columns])
 
         def fetch_last_codes(k, rows):
             nc.sync.dma_start(last_codes[k][:, rows, :], q_view[LAST, :, rows, COLUMNS[k]])
@@ -97,8 +100,10 @@ def tile_moewna16matmul_b_kernel(tc, base, state, q, scale, zp, offs, out):
         def multiply_on_gpsimd(k, rows):
             nc.gpsimd.tensor_tensor(
                 w[GPSIMD_EXPERT][k][:, rows, :],
-                codes[GPSIMD_EXPERT, rows.start][:, :, COLUMNS[k]],
-                scales[:, GPSIMD_EXPERT : GPSIMD_EXPERT + 1, COLUMNS[k]].to_broadcast([P, R // 2, BANK]),
+                codes_of(GPSIMD_EXPERT, rows)[:, :, COLUMNS[k]],
+                scales[:, GPSIMD_EXPERT : GPSIMD_EXPERT + 1, COLUMNS[k]].to_broadcast(
+                    [P, rows.stop - rows.start, BANK]
+                ),
                 MULT,
             )
 
@@ -137,8 +142,9 @@ def tile_moewna16matmul_b_kernel(tc, base, state, q, scale, zp, offs, out):
             return main, corr
 
         fetch_scales(ALL_BUT_LAST)
-        fetch_codes(GPSIMD_EXPERT, LOW)
-        fetch_codes(FIRST, LOW)
+        for rows in QUARTERS:
+            fetch_codes(GPSIMD_EXPERT, rows)
+            fetch_codes(FIRST, rows)
         fetch_codes(FIRST, HIGH)
         fetch_zp(ALL_BUT_LAST)
         fetch_codes(SECOND, LOW)
@@ -152,6 +158,7 @@ def tile_moewna16matmul_b_kernel(tc, base, state, q, scale, zp, offs, out):
         fetch_codes(GPSIMD_EXPERT, HIGH, UPPER)
         fetch_last_codes(1, LOW)
         fetch_last_codes(1, HIGH)
+        nc.sync.dma_start(offsets[:], offs)
 
         identity32 = held.tile([P, P], F32, name="identity32")
         masks.make_identity(nc, identity32[:])
@@ -159,15 +166,15 @@ def tile_moewna16matmul_b_kernel(tc, base, state, q, scale, zp, offs, out):
         masks.make_identity(nc, identity[:])
 
         scale_banks = {e: scales_to_psum(e) for e in VECTOR_EXPERTS}
-        for e in (FIRST, SECOND):
-            for rows in (LOW, HIGH):
-                for k in range(BANKS_OF_SCALES):
-                    multiply_on_vector(e, k, rows, codes[e, rows.start][:, :, COLUMNS[k]])
+        for e, rows in [(FIRST, rows) for rows in QUARTERS + (HIGH,)] + [(SECOND, LOW), (SECOND, HIGH)]:
+            for k in range(BANKS_OF_SCALES):
+                multiply_on_vector(e, k, rows, codes_of(e, rows)[:, :, COLUMNS[k]])
         multiply_on_vector(LAST, 0, ALL_ROWS, last_codes[0][:])
         for rows in (LOW, HIGH):
             multiply_on_vector(LAST, 1, rows, last_codes[1][:, rows, :])
-        for k in range(BANKS_OF_SCALES):
-            multiply_on_gpsimd(k, LOW)
+        for rows in QUARTERS:
+            for k in range(BANKS_OF_SCALES):
+                multiply_on_gpsimd(k, rows)
         nz_on_gpsimd(ALL_BUT_LAST)
         nz_on_gpsimd(ONLY_LAST)
         for k in range(BANKS_OF_SCALES):

@@ -53,10 +53,6 @@ def tile_moewna16matmul_b_kernel(tc, base, state, q, scale, zp, offs, out):
                 codes[e, rows.start // LOW.stop] = streamed.tile([P, R // 2, C], BF16, name="codes", tag="streamed")
         last_codes = [streamed.tile([P, R, BANK], BF16, name="last_codes", tag="streamed") for k in range(2)]
 
-        def fetch_scales(experts):
-            nc.sync.dma_start(scales[:, experts, :], scale_view[:, experts, :])
-            nc.scalar.mul(minus_scales[:, experts, :], scales[:, experts, :], -1.0)
-
         def codes_of(e, rows):
             half = rows.start // LOW.stop
             return codes[e, half][:, rows.start - half * LOW.stop : rows.stop - half * LOW.stop, :]
@@ -141,7 +137,8 @@ def tile_moewna16matmul_b_kernel(tc, base, state, q, scale, zp, offs, out):
                 nc.scalar.copy(corr[:, bank * BANK : (bank + 1) * BANK], corr_ps[:])
             return main, corr
 
-        fetch_scales(ALL_BUT_LAST)
+        nc.sync.dma_start(scales[:], scale_view)
+        nc.scalar.mul(minus_scales[:], scales[:], -1.0)
         for rows in QUARTERS:
             fetch_codes(GPSIMD_EXPERT, rows)
             fetch_codes(FIRST, rows)
@@ -150,7 +147,6 @@ def tile_moewna16matmul_b_kernel(tc, base, state, q, scale, zp, offs, out):
         fetch_codes(SECOND, LOW)
         fetch_codes(SECOND, HIGH)
         fetch_tokens(0)
-        fetch_scales(ONLY_LAST)
         fetch_zp(ONLY_LAST)
         fetch_codes(GPSIMD_EXPERT, HIGH, LOWER)
         fetch_last_codes(0, ALL_ROWS)

import concourse.masks as masks
import concourse.mybir as mybir

BF16, F32, U16 = mybir.dt.bfloat16, mybir.dt.float32, mybir.dt.uint16
MULT, ADD = mybir.AluOpType.mult, mybir.AluOpType.add

P = 128
E, K, C, S, N = 4, 1024, 1024, 2048, 1024
R = K // P
H = N // E
BLOCKS = C // P
BANK = 512
BANKS_OF_SCALES = C // BANK
GPSIMD_EXPERT = 2
FIRST, SECOND, LAST = VECTOR_EXPERTS = (0, 1, 3)
ALL_BUT_LAST, ONLY_LAST = slice(0, LAST), slice(LAST, E)
ALL_ROWS, LOW, HIGH = slice(0, R), slice(0, R // 2), slice(R // 2, R)
QUARTERS = (slice(0, R // 4), slice(R // 4, R // 2))
ALL_COLUMNS = slice(0, C)
LOWER, UPPER = slice(0, BANK), slice(BANK, C)
COLUMNS = (LOWER, UPPER)
SUMS_AHEAD = 4

FLOPS = 2 * C * N * (K + P)


def tile_moewna16matmul_b_kernel(tc, base, state, q, scale, zp, offs, out):
    nc = tc.nc
    q_view = q.rearrange("e (r u) c -> e u r c", u=P)
    state_view = state.rearrange("(r u) j -> u r j", u=P)
    scale_view = scale.rearrange("e u c -> u e c")
    zp_view = zp.rearrange("e u c -> u e c")

    with (
        tc.tile_pool(name="held", bufs=1) as held,
        tc.tile_pool(name="streamed", bufs=BLOCKS) as streamed,
        tc.tile_pool(name="sums", bufs=SUMS_AHEAD) as sums_pool,
        tc.psum_pool(name="scale_psum", bufs=2 * BANKS_OF_SCALES) as scale_psum,
        tc.psum_pool(name="psum", bufs=2) as psum,
    ):
        offsets = held.tile([P, N // 16], U16, name="offsets")
        tokens = held.tile([P, R, N], BF16, name="tokens")
        scales = held.tile([P, E, C], F32, name="scales")
        minus_scales = held.tile([P, E, C], F32, name="minus_scales")
        zero_points = held.tile([P, E, C], F32, name="zero_points")
        w = [
            [held.tile([P, R, BANK], BF16, name=f"w{e}_{k}") for k in range(BANKS_OF_SCALES)] for e in range(E)
        ]
        nz = held.tile([P, E, C], BF16, name="nz")
        codes = {}
        for e in (GPSIMD_EXPERT, FIRST, SECOND):
            for rows in (LOW, HIGH):
                codes[e, rows.start // LOW.stop] = streamed.tile([P, R // 2, C], BF16, name="codes", tag="streamed")
        last_codes = [streamed.tile([P, R, BANK], BF16, name="last_codes", tag="streamed") for k in range(2)]

        def codes_of(e, rows):
            half = rows.start // LOW.stop
            return codes[e, half][:, rows.start - half * LOW.stop : rows.stop - half * LOW.stop, :]

        def fetch_codes(e, rows, columns=ALL_COLUMNS):
            nc.sync.dma_start(codes_of(e, rows)[:, :, columns], q_view[e, :, rows, columns])

        def fetch_last_codes(k, rows):
            nc.sync.dma_start(last_codes[k][:, rows, :], q_view[LAST, :, rows, COLUMNS[k]])

        def fetch_zp(experts):
            nc.sync.dma_start(zero_points[:, experts, :], zp_view[:, experts, :])

        def fetch_tokens(bank):
            columns = slice(bank * BANK, (bank + 1) * BANK)
            nc.sync.dma_start(tokens[:, :, columns], state_view[:, :, columns])

        def fetch_window(b):
            window = streamed.tile([P, S], F32, name="window", tag="streamed")
            nc.sync.dma_start(window[:], base[b * P : (b + 1) * P, :])
            return window

        def scales_to_psum(e):
            banks = []
            for k in range(BANKS_OF_SCALES):
                scale_ps = scale_psum.tile([P, 1, BANK], F32, name="scale_ps")
                nc.tensor.matmul(
                    scale_ps[:, 0, :], identity32[:], scales[:, e, k * BANK : (k + 1) * BANK], start=True, stop=True
                )
                banks.append(scale_ps)
            return banks

        def multiply_on_vector(e, k, rows, tile):
            nc.vector.tensor_tensor(
                w[e][k][:, rows, :],
                tile,
                scale_banks[e][k][:].to_broadcast([P, rows.stop - rows.start, BANK]),
                MULT,
            )

        def multiply_on_gpsimd(k, rows):
            nc.gpsimd.tensor_tensor(
                w[GPSIMD_EXPERT][k][:, rows, :],
                codes_of(GPSIMD_EXPERT, rows)[:, :, COLUMNS[k]],
                scales[:, GPSIMD_EXPERT : GPSIMD_EXPERT + 1, COLUMNS[k]].to_broadcast(
                    [P, rows.stop - rows.start, BANK]
                ),
                MULT,
            )

        def nz_on_gpsimd(experts):
            nc.gpsimd.tensor_tensor(nz[:, experts, :], zero_points[:, experts, :], minus_scales[:, experts, :], MULT)

        def sums_of_block(b):
            columns = slice(b * P, (b + 1) * P)
            k = b * P // BANK
            columns_of_w = slice(b * P - k * BANK, (b + 1) * P - k * BANK)
            main = sums_pool.tile([P, N], F32, name="main")
            corr = sums_pool.tile([P, N], F32, name="corr")
            for bank in range(N // BANK):
                main_ps = psum.tile([P, BANK], F32, name="main_ps")
                for e in (2 * bank, 2 * bank + 1):
                    for r in range(R):
                        nc.tensor.matmul(
                            main_ps[:, (e % 2) * H : (e % 2 + 1) * H],
                            w[e][k][:, r, columns_of_w],
                            tokens[:, r, e * H : (e + 1) * H],
                            start=(r == 0),
                            stop=(r == R - 1),
                        )
                nc.scalar.copy(main[:, bank * BANK : (bank + 1) * BANK], main_ps[:])
            for bank in range(N // BANK):
                corr_ps = psum.tile([P, BANK], F32, name="corr_ps")
                for e in (2 * bank, 2 * bank + 1):
                    nc.tensor.matmul(
                        corr_ps[:, (e % 2) * H : (e % 2 + 1) * H],
                        nz[:, e, columns],
                        xs[:, e * H : (e + 1) * H],
                        start=True,
                        stop=True,
                    )
                nc.scalar.copy(corr[:, bank * BANK : (bank + 1) * BANK], corr_ps[:])
            return main, corr

        nc.sync.dma_start(scales[:], scale_view)
        nc.scalar.mul(minus_scales[:], scales[:], -1.0)
        for rows in QUARTERS:
            fetch_codes(GPSIMD_EXPERT, rows)
            fetch_codes(FIRST, rows)
        fetch_codes(FIRST, HIGH)
        fetch_zp(ALL_BUT_LAST)
        fetch_codes(SECOND, LOW)
        fetch_codes(SECOND, HIGH)
        fetch_tokens(0)
        fetch_zp(ONLY_LAST)
        fetch_codes(GPSIMD_EXPERT, HIGH, LOWER)
        fetch_last_codes(0, ALL_ROWS)
        fetch_tokens(1)
        fetch_codes(GPSIMD_EXPERT, HIGH, UPPER)
        fetch_last_codes(1, LOW)
        fetch_last_codes(1, HIGH)
        nc.sync.dma_start(offsets[:], offs)

        identity32 = held.tile([P, P], F32, name="identity32")
        masks.make_identity(nc, identity32[:])
        identity = held.tile([P, P], BF16, name="identity")
        masks.make_identity(nc, identity[:])

        scale_banks = {e: scales_to_psum(e) for e in VECTOR_EXPERTS}
        for e, rows in [(FIRST, rows) for rows in QUARTERS + (HIGH,)] + [(SECOND, LOW), (SECOND, HIGH)]:
            for k in range(BANKS_OF_SCALES):
                multiply_on_vector(e, k, rows, codes_of(e, rows)[:, :, COLUMNS[k]])
        multiply_on_vector(LAST, 0, ALL_ROWS, last_codes[0][:])
        for rows in (LOW, HIGH):
            multiply_on_vector(LAST, 1, rows, last_codes[1][:, rows, :])
        for rows in QUARTERS:
            for k in range(BANKS_OF_SCALES):
                multiply_on_gpsimd(k, rows)
        nz_on_gpsimd(ALL_BUT_LAST)
        nz_on_gpsimd(ONLY_LAST)
        for k in range(BANKS_OF_SCALES):
            multiply_on_gpsimd(k, HIGH)

        xs = held.tile([P, N], BF16, name="xs")
        for bank in range(N // BANK):
            xs_ps = psum.tile([P, BANK], F32, name="xs_ps", tag="corr_ps")
            for r in range(R):
                nc.tensor.matmul(
                    xs_ps[:],
                    identity[:],
                    tokens[:, r, bank * BANK : (bank + 1) * BANK],
                    start=(r == 0),
                    stop=(r == R - 1),
                )
            nc.scalar.copy(xs[:, bank * BANK : (bank + 1) * BANK], xs_ps[:])

        sums = {b: sums_of_block(b) for b in range(SUMS_AHEAD)}

        windows = [fetch_window(b) for b in range(BLOCKS)]
        for b in range(BLOCKS):
            main, corr = sums[b]
            nc.vector.tensor_tensor(windows[b][:].indirect(offsets[:]), main[:], corr[:], ADD)
            nc.sync.dma_start(out[b * P : (b + 1) * P, :], windows[b][:])
            if b + SUMS_AHEAD < BLOCKS:
                sums[b + SUMS_AHEAD] = sums_of_block(b + SUMS_AHEAD)
